import numpy as np
import ml_dtypes


def mxq(x, axis, fmt="e4m3"):
    dtype, down = {"e4m3": (ml_dtypes.float8_e4m3fn, 7), "e5m2": (ml_dtypes.float8_e5m2, 14)}[fmt]
    v = np.moveaxis(np.asarray(x, np.float32).astype(ml_dtypes.bfloat16).astype(np.float64), axis, -1)
    blocks = v.reshape(v.shape[:-1] + (-1, 32))
    amax = np.abs(blocks).max(-1, keepdims=True)
    byte = np.maximum(np.where(amax > 0, np.frexp(amax)[1] - 1 + 127, 0) - down, 1)
    scale = np.exp2(byte - 127.0)
    codes = (blocks / scale).astype(np.float32).astype(dtype).astype(np.float64)
    return np.moveaxis((codes * scale).reshape(v.shape), -1, axis)


WIDE = False


def mx_kscale(k):
    if not WIDE:
        return np.ones(k)
    levels = np.array([10, -10, 5, -5, 0])
    a = np.random.permutation(np.resize(levels, k // 512 * 4)).reshape(k // 512, 4)
    idx = np.arange(k)
    return np.exp2(a[idx // 512, idx % 128 // 32])


BF16 = ml_dtypes.bfloat16


def bf(x):
    return np.asarray(x, np.float32).astype(BF16)


def f64(x):
    return np.asarray(x).astype(np.float64)


N, IN, HID, OUT, NB = 2048, 512, 1024, 256, 64
EPS = 1e-8


def draw_adj():
    r = np.exp(0.5 * np.random.standard_normal(N))
    u = np.random.uniform(size=(N, N)) * (np.random.uniform(size=(N, N)) < NB / N)
    return u * r[:, None] * r[None, :]


def setup_inputs():
    t = mx_kscale(IN)
    return {"x": bf(np.random.standard_normal((N, IN)) * 0.25 * np.sqrt(NB) * t[None, :]),
            "adj": bf(draw_adj()),
            "W1": bf(np.random.standard_normal((HID, IN)) * 3.0 / np.sqrt(IN) / t[None, :]),
            "b1": bf(np.random.standard_normal(HID) * 0.3)}


def reference(x, adj, W1, b1):
    a = f64(adj)
    deg = a.sum(axis=1)
    d = 1.0 / np.sqrt(deg + EPS)
    norm_adj = d[:, None] * a * d[None, :]
    agg = mxq(norm_adj, 1, "e4m3") @ mxq(f64(x), 0, "e4m3")
    return np.maximum((mxq(agg, 1, "e4m3") @ mxq(f64(W1), 1, "e4m3").T) + f64(b1), 0.0)

@@ -1,0 +1,233 @@
+from contextlib import ExitStack
+
+import concourse.mybir as mybir
+from concourse.masks import make_identity
+
+F32 = mybir.dt.float32
+BF16 = mybir.dt.bfloat16
+U32 = mybir.dt.uint32
+U8 = mybir.dt.uint8
+FP8X4 = mybir.dt.float8_e4m3fn_x4
+ALU = mybir.AluOpType
+ACT = mybir.ActivationFunctionType
+
+P = 128
+PACK = 4
+K_PASS = P * PACK
+NODES = 2048
+F_IN = 512
+F_HID = 1024
+EPS = 1e-8
+ROW_TILES = NODES // P
+NODE_PASSES = NODES // K_PASS
+HID_BLOCKS = F_HID // P
+N_MAX = 512
+FLT_MAX = 3.4028234663852886e38
+
+FLOPS = 2 * NODES * NODES * F_IN + 2 * NODES * F_IN * F_HID
+
+
+def tile_simplegcn_pa_kernel(tc, x, adj, W1, b1, out):
+    nc = tc.nc
+    with ExitStack() as ctx:
+        keep = ctx.enter_context(tc.tile_pool(name="keep", bufs=1))
+        stage = ctx.enter_context(tc.tile_pool(name="stage", bufs=2))
+        rows = ctx.enter_context(tc.tile_pool(name="rows", bufs=3))
+        psum_t = ctx.enter_context(tc.psum_pool(name="psum_t", bufs=4))
+        psum_agg = ctx.enter_context(tc.psum_pool(name="psum_agg", bufs=2))
+        psum_out = ctx.enter_context(tc.psum_pool(name="psum_out", bufs=2))
+
+        x_sb = keep.tile([P, ROW_TILES, F_IN], BF16)
+        x_view = x.rearrange("(b p) f -> p b f", p=P)
+        for g in range(NODE_PASSES):
+            blocks = slice(PACK * g, PACK * (g + 1))
+            nc.sync.dma_start(out=x_sb[:, blocks, :], in_=x_view[:, blocks, :])
+        w_sb = keep.tile([P, HID_BLOCKS, F_IN], BF16)
+        nc.sync.dma_start(out=w_sb[:], in_=W1.rearrange("(b p) f -> p b f", p=P))
+        adj_sb = keep.tile([P, ROW_TILES, NODES], BF16)
+        for r in range(ROW_TILES):
+            nc.sync.dma_start(out=adj_sb[:, r, :], in_=adj[P * r : P * (r + 1), :])
+        bias_sb = keep.tile([P, F_HID], BF16)
+        nc.sync.dma_start(out=bias_sb[:], in_=b1.partition_broadcast(P))
+
+        ident_f32 = keep.tile([P, P], F32)
+        make_identity(nc, ident_f32[:])
+        ident_bf16 = keep.tile([P, P], BF16)
+        make_identity(nc, ident_bf16[:])
+        eps_col = keep.tile([P, 1], F32)
+        nc.vector.memset(eps_col[:], EPS)
+        table_warm = keep.tile([P, 1], F32)
+        nc.scalar.activation(out=table_warm[:], in_=eps_col[:], func=ACT.Sqrt)
+
+        x_codes = keep.tile([P, NODE_PASSES, F_IN], U32, align_bytes=64)
+        x_scales = keep.tile([P, NODE_PASSES, F_IN], U8, align_bytes=64)
+
+        def group_x(g):
+            x_grouped = stage.tile([P, F_IN, PACK], BF16, align_bytes=64, name="x_grouped")
+            nc.vector.tensor_copy(
+                out=x_grouped[:].rearrange("p (c i) t -> p c t i", i=4),
+                in_=x_sb[:, PACK * g : PACK * (g + 1), :].rearrange("p t (c i) -> p c t i", i=4),
+            )
+            return x_grouped
+
+        def quantise_x(g, x_grouped):
+            nc.vector.quantize_mx(
+                out=x_codes[:, g, :].bitcast(FP8X4),
+                scales=x_scales[:, g, :],
+                in_=x_grouped[:].rearrange("p f t -> p (f t)"),
+            )
+
+        waiting = group_x(0)
+        for g in range(1, NODE_PASSES):
+            fresh = group_x(g)
+            quantise_x(g - 1, waiting)
+            waiting = fresh
+        quantise_x(NODE_PASSES - 1, waiting)
+
+        w_grouped = keep.tile([P, F_HID, PACK], BF16, align_bytes=64)
+        w_codes = keep.tile([P, F_HID], U32, align_bytes=64)
+        w_scales = keep.tile([P, F_HID], U8, align_bytes=64)
+        for hb in range(HID_BLOCKS):
+            w_t = psum_t.tile([P, PACK, P], BF16, tag="bank", name="w_t")
+            for t in range(PACK):
+                nc.tensor.transpose(w_t[:, t, :], w_sb[:, hb, P * t : P * (t + 1)], ident_bf16[:])
+            nc.scalar.copy(
+                out=w_grouped[:, P * hb : P * (hb + 1), :], in_=w_t[:].rearrange("p t h -> p h t")
+            )
+        nc.vector.quantize_mx(
+            out=w_codes[:].bitcast(FP8X4),
+            scales=w_scales[:],
+            in_=w_grouped[:].rearrange("p h t -> p (h t)"),
+        )
+
+        deg_s = keep.tile([P, ROW_TILES // 2], F32)
+        deg_v = keep.tile([P, ROW_TILES // 2], F32)
+        root = keep.tile([P, ROW_TILES // 2, 2], F32)
+        d_col = keep.tile([P, ROW_TILES], F32)
+        unused_s = keep.tile([P, NODES], BF16)
+        unused_v = keep.tile([P, NODES], BF16)
+        for wave in range(NODE_PASSES):
+            for r in range(PACK * wave, PACK * (wave + 1)):
+                pair = r // 2
+                if r % 2 == 0:
+                    nc.scalar.activation(
+                        out=unused_s[:],
+                        in_=adj_sb[:, r, :],
+                        func=ACT.Copy,
+                        accum_out=deg_s[:, pair : pair + 1],
+                    )
+                else:
+                    nc.vector.tensor_scalar(
+                        out=unused_v[:],
+                        in0=adj_sb[:, r, :],
+                        scalar1=1.0,
+                        scalar2=None,
+                        op0=ALU.mult,
+                        op1=ALU.add,
+                        accum_out=deg_v[:, pair : pair + 1],
+                    )
+            pairs = slice(2 * wave, 2 * wave + 2)
+            nc.scalar.activation(
+                out=root[:, pairs, 0], in_=deg_s[:, pairs], func=ACT.Sqrt, bias=eps_col[:, 0:1]
+            )
+            nc.scalar.activation(
+                out=root[:, pairs, 1], in_=deg_v[:, pairs], func=ACT.Sqrt, bias=eps_col[:, 0:1]
+            )
+            nc.vector.reciprocal(
+                out=d_col[:, PACK * wave : PACK * (wave + 1)],
+                in_=root[:, pairs, :].rearrange("p a b -> p (a b)"),
+            )
+
+        def prescale(r):
+            scaled = rows.tile([P, NODES], F32, name="scaled")
+            nc.scalar.activation(
+                out=scaled[:], in_=adj_sb[:, r, :], func=ACT.Copy, scale=d_col[:, r : r + 1]
+            )
+            return scaled
+
+        def normalise(scaled):
+            n_grouped = rows.tile([P, NODE_PASSES, P, PACK], BF16, align_bytes=64, name="n_grouped")
+            for g in range(NODE_PASSES):
+                bank = psum_t.tile([P, PACK, P], F32, tag="bank", name="bank")
+                for t in range(PACK):
+                    b = PACK * g + t
+                    nc.tensor.transpose(bank[:, t, :], scaled[:, P * b : P * (b + 1)], ident_f32[:])
+                nc.vector.tensor_tensor(
+                    out=n_grouped[:, g, :, :],
+                    in0=bank[:].rearrange("p t i -> p i t"),
+                    in1=d_col[:, PACK * g : PACK * (g + 1)].unsqueeze(1).to_broadcast([P, P, PACK]),
+                    op=ALU.mult,
+                )
+            return n_grouped
+
+        def quantise_n(n_grouped):
+            n_codes = rows.tile([P, NODE_PASSES, P], U32, align_bytes=64, name="n_codes")
+            n_scales = rows.tile([P, NODE_PASSES, P], U8, align_bytes=64, name="n_scales")
+            nc.vector.quantize_mx(
+                out=n_codes[:].rearrange("p g i -> p (g i)").bitcast(FP8X4),
+                scales=n_scales[:].rearrange("p g i -> p (g i)"),
+                in_=n_grouped[:].rearrange("p g i t -> p (g i t)"),
+            )
+            return n_codes, n_scales
+
+        def aggregate(n_codes, n_scales):
+            agg_t = psum_agg.tile([P, PACK, P], F32, name="agg_t")
+            for t in range(PACK):
+                f_cols = slice(P * t, P * (t + 1))
+                for g in range(NODE_PASSES):
+                    nc.tensor.matmul_mx(
+                        out=agg_t[:, t, :],
+                        lhsT=x_codes[:, g, f_cols].bitcast(FP8X4),
+                        lhsT_scale=x_scales[:, g, f_cols],
+                        rhs=n_codes[:, g, :].bitcast(FP8X4),
+                        rhs_scale=n_scales[:, g, :],
+                        start=(g == 0),
+                        stop=(g == NODE_PASSES - 1),
+                    )
+            a_grouped = rows.tile([P, P, PACK], BF16, align_bytes=64, name="a_grouped")
+            nc.scalar.copy(out=a_grouped[:], in_=agg_t[:].rearrange("p t i -> p i t"))
+            a_codes = rows.tile([P, P], U32, align_bytes=64, name="a_codes")
+            a_scales = rows.tile([P, P], U8, align_bytes=64, name="a_scales")
+            nc.vector.quantize_mx(
+                out=a_codes[:].bitcast(FP8X4),
+                scales=a_scales[:],
+                in_=a_grouped[:].rearrange("p i t -> p (i t)"),
+            )
+            return a_codes, a_scales
+
+        def hidden_layer(r, a_codes, a_scales):
+            o_sb = rows.tile([P, F_HID], F32, name="o_sb")
+            for half in range(F_HID // N_MAX):
+                h_cols = slice(N_MAX * half, N_MAX * (half + 1))
+                acc = psum_out.tile([P, N_MAX], F32, name="acc")
+                nc.tensor.matmul_mx(
+                    out=acc[:],
+                    lhsT=a_codes[:].bitcast(FP8X4),
+                    lhsT_scale=a_scales[:],
+                    rhs=w_codes[:, h_cols].bitcast(FP8X4),
+                    rhs_scale=w_scales[:, h_cols],
+                    start=True,
+                    stop=True,
+                )
+                nc.vector.tensor_tensor(
+                    out=o_sb[:, h_cols], in0=acc[:], in1=bias_sb[:, h_cols], op=ALU.add
+                )
+            nc.gpsimd.tensor_scalar(
+                out=o_sb[:], in0=o_sb[:], scalar1=FLT_MAX, scalar2=0.0, op0=ALU.min, op1=ALU.max
+            )
+            nc.sync.dma_start(out=out[P * r : P * (r + 1), :], in_=o_sb[:])
+
+        scaled = {0: prescale(0)}
+        n_mx = {}
+        a_mx = {}
+        for k in range(ROW_TILES + 2):
+            if k + 1 < ROW_TILES:
+                scaled[k + 1] = prescale(k + 1)
+            if k < ROW_TILES:
+                n_grouped = normalise(scaled[k])
+            if k >= 2:
+                hidden_layer(k - 2, a_mx[k - 2][0], a_mx[k - 2][1])
+            if k < ROW_TILES:
+                n_mx[k] = quantise_n(n_grouped)
+            if 1 <= k <= ROW_TILES:
+                a_mx[k - 1] = aggregate(n_mx[k - 1][0], n_mx[k - 1][1])

@@ -22,7 +22,7 @@ ROW_TILES = NODES // P
 NODE_PASSES = NODES // K_PASS
 HID_BLOCKS = F_HID // P
 N_MAX = 512
-FLT_MAX = 3.4028234663852886e38
+AHEAD = 6
 
 FLOPS = 2 * NODES * NODES * F_IN + 2 * NODES * F_IN * F_HID
 
@@ -33,6 +33,7 @@ def tile_simplegcn_pa_kernel(tc, x, adj, W1, b1, out):
         keep = ctx.enter_context(tc.tile_pool(name="keep", bufs=1))
         stage = ctx.enter_context(tc.tile_pool(name="stage", bufs=2))
         rows = ctx.enter_context(tc.tile_pool(name="rows", bufs=3))
+        ahead = ctx.enter_context(tc.tile_pool(name="ahead", bufs=AHEAD))
         psum_t = ctx.enter_context(tc.psum_pool(name="psum_t", bufs=4))
         psum_agg = ctx.enter_context(tc.psum_pool(name="psum_agg", bufs=2))
         psum_out = ctx.enter_context(tc.psum_pool(name="psum_out", bufs=2))
@@ -100,46 +101,39 @@ def tile_simplegcn_pa_kernel(tc, x, adj, W1, b1, out):
             in_=w_grouped[:].rearrange("p h t -> p (h t)"),
         )
 
-        deg_s = keep.tile([P, ROW_TILES // 2], F32)
-        deg_v = keep.tile([P, ROW_TILES // 2], F32)
-        root = keep.tile([P, ROW_TILES // 2, 2], F32)
+        deg_s = keep.tile([P, NODE_PASSES, 1], F32)
+        deg_v = keep.tile([P, NODE_PASSES, PACK - 1], F32)
+        root = keep.tile([P, NODE_PASSES, PACK], F32)
         d_col = keep.tile([P, ROW_TILES], F32)
         unused_s = keep.tile([P, NODES], BF16)
         unused_v = keep.tile([P, NODES], BF16)
         for wave in range(NODE_PASSES):
-            for r in range(PACK * wave, PACK * (wave + 1)):
-                pair = r // 2
-                if r % 2 == 0:
-                    nc.scalar.activation(
-                        out=unused_s[:],
-                        in_=adj_sb[:, r, :],
-                        func=ACT.Copy,
-                        accum_out=deg_s[:, pair : pair + 1],
-                    )
-                else:
-                    nc.vector.tensor_scalar(
-                        out=unused_v[:],
-                        in0=adj_sb[:, r, :],
-                        scalar1=1.0,
-                        scalar2=None,
-                        op0=ALU.mult,
-                        op1=ALU.add,
-                        accum_out=deg_v[:, pair : pair + 1],
-                    )
-            pairs = slice(2 * wave, 2 * wave + 2)
             nc.scalar.activation(
-                out=root[:, pairs, 0], in_=deg_s[:, pairs], func=ACT.Sqrt, bias=eps_col[:, 0:1]
+                out=unused_s[:],
+                in_=adj_sb[:, PACK * wave, :],
+                func=ACT.Copy,
+                accum_out=deg_s[:, wave, :],
+            )
+            for t in range(1, PACK):
+                nc.vector.tensor_scalar(
+                    out=unused_v[:],
+                    in0=adj_sb[:, PACK * wave + t, :],
+                    scalar1=1.0,
+                    scalar2=None,
+                    op0=ALU.mult,
+                    op1=ALU.add,
+                    accum_out=deg_v[:, wave, t - 1 : t],
+                )
+            nc.scalar.activation(
+                out=root[:, wave, 0:1], in_=deg_s[:, wave, :], func=ACT.Sqrt, bias=eps_col[:, 0:1]
             )
             nc.scalar.activation(
-                out=root[:, pairs, 1], in_=deg_v[:, pairs], func=ACT.Sqrt, bias=eps_col[:, 0:1]
+                out=root[:, wave, 1:PACK], in_=deg_v[:, wave, :], func=ACT.Sqrt, bias=eps_col[:, 0:1]
             )
-            nc.vector.reciprocal(
-                out=d_col[:, PACK * wave : PACK * (wave + 1)],
-                in_=root[:, pairs, :].rearrange("p a b -> p (a b)"),
-            )
+            nc.vector.reciprocal(out=d_col[:, PACK * wave : PACK * (wave + 1)], in_=root[:, wave, :])
 
         def prescale(r):
-            scaled = rows.tile([P, NODES], F32, name="scaled")
+            scaled = ahead.tile([P, NODES], F32, name="scaled")
             nc.scalar.activation(
                 out=scaled[:], in_=adj_sb[:, r, :], func=ACT.Copy, scale=d_col[:, r : r + 1]
             )
@@ -212,17 +206,17 @@ def tile_simplegcn_pa_kernel(tc, x, adj, W1, b1, out):
                 nc.vector.tensor_tensor(
                     out=o_sb[:, h_cols], in0=acc[:], in1=bias_sb[:, h_cols], op=ALU.add
                 )
-            nc.gpsimd.tensor_scalar(
-                out=o_sb[:], in0=o_sb[:], scalar1=FLT_MAX, scalar2=0.0, op0=ALU.min, op1=ALU.max
-            )
+            nc.scalar.activation(out=o_sb[:], in_=o_sb[:], func=ACT.Relu)
             nc.sync.dma_start(out=out[P * r : P * (r + 1), :], in_=o_sb[:])
 
-        scaled = {0: prescale(0)}
+        scaled = {}
+        for r in range(AHEAD - 1):
+            scaled[r] = prescale(r)
         n_mx = {}
         a_mx = {}
         for k in range(ROW_TILES + 2):
-            if k + 1 < ROW_TILES:
-                scaled[k + 1] = prescale(k + 1)
+            if k + AHEAD - 1 < ROW_TILES:
+                scaled[k + AHEAD - 1] = prescale(k + AHEAD - 1)
             if k < ROW_TILES:
                 n_grouped = normalise(scaled[k])
             if k >= 2:

@@ -34,6 +34,7 @@ def tile_simplegcn_pa_kernel(tc, x, adj, W1, b1, out):
         stage = ctx.enter_context(tc.tile_pool(name="stage", bufs=2))
         rows = ctx.enter_context(tc.tile_pool(name="rows", bufs=3))
         ahead = ctx.enter_context(tc.tile_pool(name="ahead", bufs=AHEAD))
+        outs = ctx.enter_context(tc.tile_pool(name="outs", bufs=4))
         psum_t = ctx.enter_context(tc.psum_pool(name="psum_t", bufs=4))
         psum_agg = ctx.enter_context(tc.psum_pool(name="psum_agg", bufs=2))
         psum_out = ctx.enter_context(tc.psum_pool(name="psum_out", bufs=2))
@@ -134,21 +135,32 @@ def tile_simplegcn_pa_kernel(tc, x, adj, W1, b1, out):
 
         def prescale(r):
             scaled = ahead.tile([P, NODES], F32, name="scaled")
-            nc.scalar.activation(
-                out=scaled[:], in_=adj_sb[:, r, :], func=ACT.Copy, scale=d_col[:, r : r + 1]
+            nc.gpsimd.tensor_scalar(
+                out=scaled[:],
+                in0=adj_sb[:, r, :],
+                scalar1=d_col[:, r : r + 1],
+                scalar2=0.0,
+                op0=ALU.mult,
+                op1=ALU.add,
             )
             return scaled
 
-        def normalise(scaled):
-            n_grouped = rows.tile([P, NODE_PASSES, P, PACK], BF16, align_bytes=64, name="n_grouped")
+        def transpose_row_tile(scaled):
+            banks = []
             for g in range(NODE_PASSES):
                 bank = psum_t.tile([P, PACK, P], F32, tag="bank", name="bank")
                 for t in range(PACK):
                     b = PACK * g + t
                     nc.tensor.transpose(bank[:, t, :], scaled[:, P * b : P * (b + 1)], ident_f32[:])
+                banks.append(bank)
+            return banks
+
+        def scale_columns(banks):
+            n_grouped = rows.tile([P, NODE_PASSES, P, PACK], BF16, align_bytes=64, name="n_grouped")
+            for g in range(NODE_PASSES):
                 nc.vector.tensor_tensor(
                     out=n_grouped[:, g, :, :],
-                    in0=bank[:].rearrange("p t i -> p i t"),
+                    in0=banks[g][:].rearrange("p t i -> p i t"),
                     in1=d_col[:, PACK * g : PACK * (g + 1)].unsqueeze(1).to_broadcast([P, P, PACK]),
                     op=ALU.mult,
                 )
@@ -180,6 +192,9 @@ def tile_simplegcn_pa_kernel(tc, x, adj, W1, b1, out):
                     )
             a_grouped = rows.tile([P, P, PACK], BF16, align_bytes=64, name="a_grouped")
             nc.scalar.copy(out=a_grouped[:], in_=agg_t[:].rearrange("p t i -> p i t"))
+            return a_grouped
+
+        def quantise_agg(a_grouped):
             a_codes = rows.tile([P, P], U32, align_bytes=64, name="a_codes")
             a_scales = rows.tile([P, P], U8, align_bytes=64, name="a_scales")
             nc.vector.quantize_mx(
@@ -189,8 +204,8 @@ def tile_simplegcn_pa_kernel(tc, x, adj, W1, b1, out):
             )
             return a_codes, a_scales
 
-        def hidden_layer(r, a_codes, a_scales):
-            o_sb = rows.tile([P, F_HID], F32, name="o_sb")
+        def hidden_layer(a_codes, a_scales):
+            o_sb = outs.tile([P, F_HID], F32, name="o_sb")
             for half in range(F_HID // N_MAX):
                 h_cols = slice(N_MAX * half, N_MAX * (half + 1))
                 acc = psum_out.tile([P, N_MAX], F32, name="acc")
@@ -206,22 +221,40 @@ def tile_simplegcn_pa_kernel(tc, x, adj, W1, b1, out):
                 nc.vector.tensor_tensor(
                     out=o_sb[:, h_cols], in0=acc[:], in1=bias_sb[:, h_cols], op=ALU.add
                 )
+            return o_sb
+
+        def relu_and_store(r, o_sb):
             nc.scalar.activation(out=o_sb[:], in_=o_sb[:], func=ACT.Relu)
             nc.sync.dma_start(out=out[P * r : P * (r + 1), :], in_=o_sb[:])
 
+        def is_row_tile(r):
+            return 0 <= r < ROW_TILES
+
         scaled = {}
+        banks = {}
+        n_grouped = {}
+        n_mx = {}
+        a_grouped = {}
+        a_mx = {}
+        o_sb = {}
         for r in range(AHEAD - 1):
             scaled[r] = prescale(r)
-        n_mx = {}
-        a_mx = {}
-        for k in range(ROW_TILES + 2):
-            if k + AHEAD - 1 < ROW_TILES:
-                scaled[k + AHEAD - 1] = prescale(k + AHEAD - 1)
-            if k < ROW_TILES:
-                n_grouped = normalise(scaled[k])
-            if k >= 2:
-                hidden_layer(k - 2, a_mx[k - 2][0], a_mx[k - 2][1])
-            if k < ROW_TILES:
-                n_mx[k] = quantise_n(n_grouped)
-            if 1 <= k <= ROW_TILES:
-                a_mx[k - 1] = aggregate(n_mx[k - 1][0], n_mx[k - 1][1])
+        with tc.manual_schedule():
+            pipeline_steps = range(-1, ROW_TILES + 3)
+            for k in pipeline_steps:
+                if is_row_tile(k - 3):
+                    relu_and_store(k - 3, o_sb[k - 3])
+                if is_row_tile(k):
+                    n_grouped[k] = scale_columns(banks[k])
+                if is_row_tile(k - 1):
+                    a_grouped[k - 1] = aggregate(n_mx[k - 1][0], n_mx[k - 1][1])
+                if is_row_tile(k - 2):
+                    o_sb[k - 2] = hidden_layer(a_mx[k - 2][0], a_mx[k - 2][1])
+                if is_row_tile(k + 1):
+                    banks[k + 1] = transpose_row_tile(scaled[k + 1])
+                if is_row_tile(k + AHEAD):
+                    scaled[k + AHEAD] = prescale(k + AHEAD)
+                if is_row_tile(k):
+                    n_mx[k] = quantise_n(n_grouped[k])
+                if is_row_tile(k - 1):
+                    a_mx[k - 1] = quantise_agg(a_grouped[k - 1])

@@ -224,8 +224,10 @@ def tile_simplegcn_pa_kernel(tc, x, adj, W1, b1, out):
             return o_sb
 
         def relu_and_store(r, o_sb):
-            nc.scalar.activation(out=o_sb[:], in_=o_sb[:], func=ACT.Relu)
-            nc.sync.dma_start(out=out[P * r : P * (r + 1), :], in_=o_sb[:])
+            for half in range(F_HID // N_MAX):
+                h_cols = slice(N_MAX * half, N_MAX * (half + 1))
+                nc.scalar.activation(out=o_sb[:, h_cols], in_=o_sb[:, h_cols], func=ACT.Relu)
+                nc.sync.dma_start(out=out[P * r : P * (r + 1), h_cols], in_=o_sb[:, h_cols])
 
         def is_row_tile(r):
             return 0 <= r < ROW_TILES
@@ -246,10 +248,10 @@ def tile_simplegcn_pa_kernel(tc, x, adj, W1, b1, out):
                     relu_and_store(k - 3, o_sb[k - 3])
                 if is_row_tile(k):
                     n_grouped[k] = scale_columns(banks[k])
-                if is_row_tile(k - 1):
-                    a_grouped[k - 1] = aggregate(n_mx[k - 1][0], n_mx[k - 1][1])
                 if is_row_tile(k - 2):
                     o_sb[k - 2] = hidden_layer(a_mx[k - 2][0], a_mx[k - 2][1])
+                if is_row_tile(k - 1):
+                    a_grouped[k - 1] = aggregate(n_mx[k - 1][0], n_mx[k - 1][1])
                 if is_row_tile(k + 1):
                     banks[k + 1] = transpose_row_tile(scaled[k + 1])
                 if is_row_tile(k + AHEAD):

@@ -36,8 +36,8 @@ def tile_simplegcn_pa_kernel(tc, x, adj, W1, b1, out):
         ahead = ctx.enter_context(tc.tile_pool(name="ahead", bufs=AHEAD))
         outs = ctx.enter_context(tc.tile_pool(name="outs", bufs=4))
         psum_t = ctx.enter_context(tc.psum_pool(name="psum_t", bufs=4))
-        psum_agg = ctx.enter_context(tc.psum_pool(name="psum_agg", bufs=2))
-        psum_out = ctx.enter_context(tc.psum_pool(name="psum_out", bufs=2))
+        psum_agg = ctx.enter_context(tc.psum_pool(name="psum_agg", bufs=1))
+        psum_out = ctx.enter_context(tc.psum_pool(name="psum_out", bufs=1))
 
         x_sb = keep.tile([P, ROW_TILES, F_IN], BF16)
         x_view = x.rearrange("(b p) f -> p b f", p=P)
@@ -204,30 +204,56 @@ def tile_simplegcn_pa_kernel(tc, x, adj, W1, b1, out):
             )
             return a_codes, a_scales
 
-        def hidden_layer(a_codes, a_scales):
+        def hidden_direct(a_codes, a_scales):
             o_sb = outs.tile([P, F_HID], F32, name="o_sb")
-            for half in range(F_HID // N_MAX):
-                h_cols = slice(N_MAX * half, N_MAX * (half + 1))
-                acc = psum_out.tile([P, N_MAX], F32, name="acc")
+            acc = psum_out.tile([P, N_MAX], F32, name="acc")
+            nc.tensor.matmul_mx(
+                out=acc[:],
+                lhsT=a_codes[:].bitcast(FP8X4),
+                lhsT_scale=a_scales[:],
+                rhs=w_codes[:, 0:N_MAX].bitcast(FP8X4),
+                rhs_scale=w_scales[:, 0:N_MAX],
+                start=True,
+                stop=True,
+            )
+            nc.vector.tensor_tensor(
+                out=o_sb[:, 0:N_MAX], in0=acc[:], in1=bias_sb[:, 0:N_MAX], op=ALU.add
+            )
+            return o_sb
+
+        def hidden_turned(a_codes, a_scales):
+            acc_t = psum_out.tile([P, PACK, P], F32, name="acc_t")
+            for c in range(PACK):
+                h_cols = slice(N_MAX + P * c, N_MAX + P * (c + 1))
                 nc.tensor.matmul_mx(
-                    out=acc[:],
-                    lhsT=a_codes[:].bitcast(FP8X4),
-                    lhsT_scale=a_scales[:],
-                    rhs=w_codes[:, h_cols].bitcast(FP8X4),
-                    rhs_scale=w_scales[:, h_cols],
+                    out=acc_t[:, c, :],
+                    lhsT=w_codes[:, h_cols].bitcast(FP8X4),
+                    lhsT_scale=w_scales[:, h_cols],
+                    rhs=a_codes[:].bitcast(FP8X4),
+                    rhs_scale=a_scales[:],
                     start=True,
                     stop=True,
                 )
-                nc.vector.tensor_tensor(
-                    out=o_sb[:, h_cols], in0=acc[:], in1=bias_sb[:, h_cols], op=ALU.add
+            o_t = rows.tile([P, PACK, P], F32, name="o_t")
+            for c in range(PACK):
+                nc.scalar.activation(
+                    out=o_t[:, c, :], in_=acc_t[:, c, :], func=ACT.Relu, bias=b_col[:, c : c + 1]
                 )
-            return o_sb
+            return o_t
 
-        def relu_and_store(r, o_sb):
-            for half in range(F_HID // N_MAX):
-                h_cols = slice(N_MAX * half, N_MAX * (half + 1))
-                nc.scalar.activation(out=o_sb[:, h_cols], in_=o_sb[:, h_cols], func=ACT.Relu)
-                nc.sync.dma_start(out=out[P * r : P * (r + 1), h_cols], in_=o_sb[:, h_cols])
+        def turn_back(o_t):
+            back = psum_out.tile([P, PACK, P], F32, tag="back", name="back")
+            for c in range(PACK):
+                nc.tensor.transpose(back[:, c, :], o_t[:, c, :], ident_f32[:])
+            return back
+
+        def finish_direct(r, o_sb):
+            nc.scalar.activation(out=o_sb[:, 0:N_MAX], in_=o_sb[:, 0:N_MAX], func=ACT.Relu)
+            nc.sync.dma_start(out=out[P * r : P * (r + 1), 0:N_MAX], in_=o_sb[:, 0:N_MAX])
+
+        def finish_turned(r, o_sb, back):
+            nc.scalar.copy(out=o_sb[:, N_MAX:F_HID], in_=back[:].rearrange("p c h -> p (c h)"))
+            nc.sync.dma_start(out=out[P * r : P * (r + 1), N_MAX:F_HID], in_=o_sb[:, N_MAX:F_HID])
 
         def is_row_tile(r):
             return 0 <= r < ROW_TILES
@@ -239,21 +265,34 @@ def tile_simplegcn_pa_kernel(tc, x, adj, W1, b1, out):
         a_grouped = {}
         a_mx = {}
         o_sb = {}
+        o_t = {}
+        back = {}
+        b_col = keep.tile([P, PACK], F32)
         for r in range(AHEAD - 1):
             scaled[r] = prescale(r)
         with tc.manual_schedule():
+            b_t = psum_out.tile([P, PACK, P], BF16, tag="back", name="b_t")
+            for c in range(PACK):
+                nc.tensor.transpose(
+                    b_t[:, c, :], bias_sb[:, N_MAX + P * c : N_MAX + P * (c + 1)], ident_bf16[:]
+                )
+            nc.vector.tensor_copy(out=b_col[:], in_=b_t[:, :, 0])
             pipeline_steps = range(-1, ROW_TILES + 3)
             for k in pipeline_steps:
-                if is_row_tile(k - 3):
-                    relu_and_store(k - 3, o_sb[k - 3])
                 if is_row_tile(k):
                     n_grouped[k] = scale_columns(banks[k])
                 if is_row_tile(k - 2):
-                    o_sb[k - 2] = hidden_layer(a_mx[k - 2][0], a_mx[k - 2][1])
+                    o_sb[k - 2] = hidden_direct(a_mx[k - 2][0], a_mx[k - 2][1])
+                    o_t[k - 2] = hidden_turned(a_mx[k - 2][0], a_mx[k - 2][1])
                 if is_row_tile(k - 1):
                     a_grouped[k - 1] = aggregate(n_mx[k - 1][0], n_mx[k - 1][1])
+                if is_row_tile(k - 3):
+                    finish_direct(k - 3, o_sb[k - 3])
+                    back[k - 3] = turn_back(o_t[k - 3])
                 if is_row_tile(k + 1):
                     banks[k + 1] = transpose_row_tile(scaled[k + 1])
+                if is_row_tile(k - 3):
+                    finish_turned(k - 3, o_sb[k - 3], back[k - 3])
                 if is_row_tile(k + AHEAD):
                     scaled[k + AHEAD] = prescale(k + AHEAD)
                 if is_row_tile(k):

@@ -281,11 +281,11 @@ def tile_simplegcn_pa_kernel(tc, x, adj, W1, b1, out):
             for k in pipeline_steps:
                 if is_row_tile(k):
                     n_grouped[k] = scale_columns(banks[k])
+                if is_row_tile(k - 1):
+                    a_grouped[k - 1] = aggregate(n_mx[k - 1][0], n_mx[k - 1][1])
                 if is_row_tile(k - 2):
                     o_sb[k - 2] = hidden_direct(a_mx[k - 2][0], a_mx[k - 2][1])
                     o_t[k - 2] = hidden_turned(a_mx[k - 2][0], a_mx[k - 2][1])
-                if is_row_tile(k - 1):
-                    a_grouped[k - 1] = aggregate(n_mx[k - 1][0], n_mx[k - 1][1])
                 if is_row_tile(k - 3):
                     finish_direct(k - 3, o_sb[k - 3])
                     back[k - 3] = turn_back(o_t[k - 3])

@@ -22,6 +22,7 @@ ROW_TILES = NODES // P
 NODE_PASSES = NODES // K_PASS
 HID_BLOCKS = F_HID // P
 N_MAX = 512
+SPLIT = NODES - K_PASS
 AHEAD = 6
 
 FLOPS = 2 * NODES * NODES * F_IN + 2 * NODES * F_IN * F_HID
@@ -136,12 +137,15 @@ def tile_simplegcn_pa_kernel(tc, x, adj, W1, b1, out):
         def prescale(r):
             scaled = ahead.tile([P, NODES], F32, name="scaled")
             nc.gpsimd.tensor_scalar(
-                out=scaled[:],
-                in0=adj_sb[:, r, :],
+                out=scaled[:, 0:SPLIT],
+                in0=adj_sb[:, r, 0:SPLIT],
                 scalar1=d_col[:, r : r + 1],
                 scalar2=0.0,
                 op0=ALU.mult,
                 op1=ALU.add,
+            )
+            nc.scalar.activation(
+                out=scaled[:, SPLIT:NODES], in_=adj_sb[:, r, SPLIT:NODES], func=ACT.Copy, scale=d_col[:, r : r + 1]
             )
             return scaled
 

@@ -10,6 +10,7 @@ U8 = mybir.dt.uint8
 FP8X4 = mybir.dt.float8_e4m3fn_x4
 ALU = mybir.AluOpType
 ACT = mybir.ActivationFunctionType
+AXL = mybir.AxisListType
 
 P = 128
 PACK = 4
@@ -22,8 +23,13 @@ ROW_TILES = NODES // P
 NODE_PASSES = NODES // K_PASS
 HID_BLOCKS = F_HID // P
 N_MAX = 512
-SPLIT = NODES - K_PASS
-AHEAD = 6
+LOADS = ("a0", "a1", "x0", "x1", "a2", "a3", "x2", "x3", "w0", "w1")
+PER_STEP = 3
+TC = 2
+DIRECT = F_HID - P * TC
+SUMS = ("VVVV", "VVPP", "PPSP", "PPSP")
+X_ENG = 'SVSV'
+DROW = "S"
 
 FLOPS = 2 * NODES * NODES * F_IN + 2 * NODES * F_IN * F_HID
 
@@ -32,24 +38,35 @@ def tile_simplegcn_pa_kernel(tc, x, adj, W1, b1, out):
     nc = tc.nc
     with ExitStack() as ctx:
         keep = ctx.enter_context(tc.tile_pool(name="keep", bufs=1))
-        stage = ctx.enter_context(tc.tile_pool(name="stage", bufs=2))
+        io = ctx.enter_context(tc.tile_pool(name="io", bufs=6))
+        stage = ctx.enter_context(tc.tile_pool(name="stage", bufs=4))
         rows = ctx.enter_context(tc.tile_pool(name="rows", bufs=3))
-        ahead = ctx.enter_context(tc.tile_pool(name="ahead", bufs=AHEAD))
-        outs = ctx.enter_context(tc.tile_pool(name="outs", bufs=4))
-        psum_t = ctx.enter_context(tc.psum_pool(name="psum_t", bufs=4))
+        psum_t = ctx.enter_context(tc.psum_pool(name="psum_t", bufs=3))
         psum_agg = ctx.enter_context(tc.psum_pool(name="psum_agg", bufs=1))
-        psum_out = ctx.enter_context(tc.psum_pool(name="psum_out", bufs=1))
+        psum_side = ctx.enter_context(tc.psum_pool(name="psum_side", bufs=1))
+        psum_out = ctx.enter_context(tc.psum_pool(name="psum_out", bufs=2))
+        ctx.enter_context(tc.manual_schedule())
 
-        x_sb = keep.tile([P, ROW_TILES, F_IN], BF16)
-        x_view = x.rearrange("(b p) f -> p b f", p=P)
-        for g in range(NODE_PASSES):
-            blocks = slice(PACK * g, PACK * (g + 1))
-            nc.sync.dma_start(out=x_sb[:, blocks, :], in_=x_view[:, blocks, :])
-        w_sb = keep.tile([P, HID_BLOCKS, F_IN], BF16)
-        nc.sync.dma_start(out=w_sb[:], in_=W1.rearrange("(b p) f -> p b f", p=P))
+        x_view = x.rearrange("(g u p e) f -> p g u e f", p=P, u=2, e=2)
+        w_view = W1.rearrange("(b p) f -> p b f", p=P)
+        x_sb = {}
+        w_sb = {}
         adj_sb = keep.tile([P, ROW_TILES, NODES], BF16)
-        for r in range(ROW_TILES):
-            nc.sync.dma_start(out=adj_sb[:, r, :], in_=adj[P * r : P * (r + 1), :])
+
+        def load_x(g):
+            x_sb[g] = io.tile([P, 2, 2, F_IN], BF16, tag="io", name="x_raw")
+            nc.sync.dma_start(out=x_sb[g][:], in_=x_view[:, g, :, :, :])
+
+        def load_w(h):
+            w_sb[h] = io.tile([P, PACK, F_IN], BF16, tag="io", name="w_raw")
+            nc.sync.dma_start(out=w_sb[h][:], in_=w_view[:, PACK * h : PACK * (h + 1), :])
+
+        def load_adj(w):
+            for r in range(PACK * w, PACK * (w + 1)):
+                nc.sync.dma_start(out=adj_sb[:, r, :], in_=adj[P * r : P * (r + 1), :])
+
+        for item in LOADS:
+            {"x": load_x, "w": load_w, "a": load_adj}[item[0]](int(item[1]))
         bias_sb = keep.tile([P, F_HID], BF16)
         nc.sync.dma_start(out=bias_sb[:], in_=b1.partition_broadcast(P))
 
@@ -67,10 +84,16 @@ def tile_simplegcn_pa_kernel(tc, x, adj, W1, b1, out):
 
         def group_x(g):
             x_grouped = stage.tile([P, F_IN, PACK], BF16, align_bytes=64, name="x_grouped")
-            nc.vector.tensor_copy(
-                out=x_grouped[:].rearrange("p (c i) t -> p c t i", i=4),
-                in_=x_sb[:, PACK * g : PACK * (g + 1), :].rearrange("p t (c i) -> p c t i", i=4),
-            )
+            dst = x_grouped[:].rearrange("p (c i) t -> p c t i", i=4)
+            src = x_sb[g][:].rearrange("p u e (c i) -> p c (u e) i", i=4)
+            if X_ENG[g] == "S":
+                nc.scalar.copy(out=dst, in_=src)
+            elif X_ENG[g] == "V":
+                nc.vector.tensor_copy(out=dst, in_=src)
+            else:
+                nc.gpsimd.tensor_scalar(
+                    out=dst, in0=src, scalar1=1.0, scalar2=0.0, op0=ALU.mult, op1=ALU.add
+                )
             return x_grouped
 
         def quantise_x(g, x_grouped):
@@ -80,108 +103,130 @@ def tile_simplegcn_pa_kernel(tc, x, adj, W1, b1, out):
                 in_=x_grouped[:].rearrange("p f t -> p (f t)"),
             )
 
-        waiting = group_x(0)
-        for g in range(1, NODE_PASSES):
-            fresh = group_x(g)
-            quantise_x(g - 1, waiting)
-            waiting = fresh
-        quantise_x(NODE_PASSES - 1, waiting)
-
         w_grouped = keep.tile([P, F_HID, PACK], BF16, align_bytes=64)
         w_codes = keep.tile([P, F_HID], U32, align_bytes=64)
         w_scales = keep.tile([P, F_HID], U8, align_bytes=64)
-        for hb in range(HID_BLOCKS):
+
+        def turn_w(hb):
             w_t = psum_t.tile([P, PACK, P], BF16, tag="bank", name="w_t")
             for t in range(PACK):
-                nc.tensor.transpose(w_t[:, t, :], w_sb[:, hb, P * t : P * (t + 1)], ident_bf16[:])
+                nc.tensor.transpose(
+                    w_t[:, t, :], w_sb[hb // PACK][:, hb % PACK, P * t : P * (t + 1)], ident_bf16[:]
+                )
             nc.scalar.copy(
                 out=w_grouped[:, P * hb : P * (hb + 1), :], in_=w_t[:].rearrange("p t h -> p h t")
             )
-        nc.vector.quantize_mx(
-            out=w_codes[:].bitcast(FP8X4),
-            scales=w_scales[:],
-            in_=w_grouped[:].rearrange("p h t -> p (h t)"),
-        )
 
-        deg_s = keep.tile([P, NODE_PASSES, 1], F32)
-        deg_v = keep.tile([P, NODE_PASSES, PACK - 1], F32)
-        root = keep.tile([P, NODE_PASSES, PACK], F32)
+        def quantise_w():
+            nc.vector.quantize_mx(
+                out=w_codes[:].bitcast(FP8X4),
+                scales=w_scales[:],
+                in_=w_grouped[:].rearrange("p h t -> p (h t)"),
+            )
+
+        deg = keep.tile([P, ROW_TILES], F32)
+        root = keep.tile([P, ROW_TILES], F32)
         d_col = keep.tile([P, ROW_TILES], F32)
+        d_row = keep.tile([P, NODES], F32)
         unused_s = keep.tile([P, NODES], BF16)
         unused_v = keep.tile([P, NODES], BF16)
-        for wave in range(NODE_PASSES):
-            nc.scalar.activation(
-                out=unused_s[:],
-                in_=adj_sb[:, PACK * wave, :],
-                func=ACT.Copy,
-                accum_out=deg_s[:, wave, :],
-            )
-            for t in range(1, PACK):
+
+        def rowsum(r, part):
+            e = SUMS[r // PACK][r % PACK]
+            if e == "S":
+                nc.scalar.activation(
+                    out=unused_s[:], in_=adj_sb[:, r, :], func=ACT.Copy, accum_out=deg[:, r : r + 1]
+                )
+            elif e == "V":
                 nc.vector.tensor_scalar(
                     out=unused_v[:],
-                    in0=adj_sb[:, PACK * wave + t, :],
+                    in0=adj_sb[:, r, :],
                     scalar1=1.0,
                     scalar2=None,
                     op0=ALU.mult,
                     op1=ALU.add,
-                    accum_out=deg_v[:, wave, t - 1 : t],
+                    accum_out=deg[:, r : r + 1],
                 )
-            nc.scalar.activation(
-                out=root[:, wave, 0:1], in_=deg_s[:, wave, :], func=ACT.Sqrt, bias=eps_col[:, 0:1]
-            )
-            nc.scalar.activation(
-                out=root[:, wave, 1:PACK], in_=deg_v[:, wave, :], func=ACT.Sqrt, bias=eps_col[:, 0:1]
-            )
-            nc.vector.reciprocal(out=d_col[:, PACK * wave : PACK * (wave + 1)], in_=root[:, wave, :])
+            else:
+                for b in range(ROW_TILES):
+                    nc.tensor.matmul(
+                        part[:, r % PACK, :],
+                        lhsT=ident_bf16[:],
+                        rhs=adj_sb[:, r, P * b : P * (b + 1)],
+                        start=(b == 0),
+                        stop=(b == ROW_TILES - 1),
+                    )
 
-        def prescale(r):
-            scaled = ahead.tile([P, NODES], F32, name="scaled")
-            nc.gpsimd.tensor_scalar(
-                out=scaled[:, 0:SPLIT],
-                in0=adj_sb[:, r, 0:SPLIT],
-                scalar1=d_col[:, r : r + 1],
-                scalar2=0.0,
+        def reduce_parts(w, part):
+            for t in range(PACK):
+                if SUMS[w][t] == "P":
+                    nc.vector.tensor_reduce(
+                        out=deg[:, PACK * w + t : PACK * w + t + 1], in_=part[:, t, :], axis=AXL.X, op=ALU.add
+                    )
+
+        def factor(w):
+            cols = slice(PACK * w, PACK * (w + 1))
+            nc.scalar.activation(out=root[:, cols], in_=deg[:, cols], func=ACT.Sqrt, bias=eps_col[:, 0:1])
+            nc.vector.reciprocal(out=d_col[:, cols], in_=root[:, cols])
+
+        def spread(w):
+            bank = psum_t.tile([P, PACK, P], F32, tag="bank", name="bank")
+            for t in range(PACK):
+                r = PACK * w + t
+                nc.tensor.transpose(
+                    bank[:, t, :], d_col[:, r : r + 1].to_broadcast([P, P]), ident_f32[:]
+                )
+            dst = d_row[:, K_PASS * w : K_PASS * (w + 1)]
+            src = bank[:].rearrange("p t n -> p (t n)")
+            if DROW == "S":
+                nc.scalar.copy(out=dst, in_=src)
+            else:
+                nc.vector.tensor_copy(out=dst, in_=src)
+
+        def normalise(r, w0, w1):
+            cols = slice(K_PASS * w0, K_PASS * w1)
+            nc.vector.scalar_tensor_tensor(
+                out=adj_sb[:, r, cols],
+                in0=adj_sb[:, r, cols],
+                scalar=d_col[:, r : r + 1],
+                in1=d_row[:, cols],
                 op0=ALU.mult,
-                op1=ALU.add,
+                op1=ALU.mult,
             )
-            nc.scalar.activation(
-                out=scaled[:, SPLIT:NODES], in_=adj_sb[:, r, SPLIT:NODES], func=ACT.Copy, scale=d_col[:, r : r + 1]
+
+        n_grouped, n_mx, a_grouped, a_mx, accs, o_sb = {}, {}, {}, {}, {}, {}
+
+        def turn_half(r, h):
+            if r not in n_grouped:
+                n_grouped[r] = rows.tile([P, NODE_PASSES, P, PACK], BF16, align_bytes=64, name="n_grouped")
+            words = adj_sb[:, r, :].bitcast(F32)
+            bank = psum_t.tile([P, PACK, P], F32, tag="bank", name="bank")
+            for q in range(PACK):
+                b = PACK * h + q
+                nc.tensor.transpose(bank[:, q, :], words[:, P * b : P * (b + 1)], ident_f32[:])
+            dst = n_grouped[r][:, 2 * h : 2 * h + 2, :, :].rearrange("p g i t -> p (g i t)").bitcast(F32)
+            nc.scalar.copy(
+                out=dst.rearrange("p (g i u) -> p g i u", g=2, u=2),
+                in_=bank[:].rearrange("p (g u) i -> p g i u", u=2),
             )
-            return scaled
 
-        def transpose_row_tile(scaled):
-            banks = []
-            for g in range(NODE_PASSES):
-                bank = psum_t.tile([P, PACK, P], F32, tag="bank", name="bank")
-                for t in range(PACK):
-                    b = PACK * g + t
-                    nc.tensor.transpose(bank[:, t, :], scaled[:, P * b : P * (b + 1)], ident_f32[:])
-                banks.append(bank)
-            return banks
+        def turn(r):
+            turn_half(r, 0)
+            turn_half(r, 1)
 
-        def scale_columns(banks):
-            n_grouped = rows.tile([P, NODE_PASSES, P, PACK], BF16, align_bytes=64, name="n_grouped")
-            for g in range(NODE_PASSES):
-                nc.vector.tensor_tensor(
-                    out=n_grouped[:, g, :, :],
-                    in0=banks[g][:].rearrange("p t i -> p i t"),
-                    in1=d_col[:, PACK * g : PACK * (g + 1)].unsqueeze(1).to_broadcast([P, P, PACK]),
-                    op=ALU.mult,
-                )
-            return n_grouped
-
-        def quantise_n(n_grouped):
-            n_codes = rows.tile([P, NODE_PASSES, P], U32, align_bytes=64, name="n_codes")
-            n_scales = rows.tile([P, NODE_PASSES, P], U8, align_bytes=64, name="n_scales")
+        def quantise_n(r):
+            codes = rows.tile([P, NODE_PASSES, P], U32, align_bytes=64, name="n_codes")
+            scales = rows.tile([P, NODE_PASSES, P], U8, align_bytes=64, name="n_scales")
             nc.vector.quantize_mx(
-                out=n_codes[:].rearrange("p g i -> p (g i)").bitcast(FP8X4),
-                scales=n_scales[:].rearrange("p g i -> p (g i)"),
-                in_=n_grouped[:].rearrange("p g i t -> p (g i t)"),
+                out=codes[:].rearrange("p g i -> p (g i)").bitcast(FP8X4),
+                scales=scales[:].rearrange("p g i -> p (g i)"),
+                in_=n_grouped[r][:].rearrange("p g i t -> p (g i t)"),
             )
-            return n_codes, n_scales
+            n_mx[r] = (codes, scales)
 
-        def aggregate(n_codes, n_scales):
-            agg_t = psum_agg.tile([P, PACK, P], F32, name="agg_t")
+        def aggregate(r):
+            codes, scales = n_mx[r]
+            agg_t = psum_agg.tile([P, PACK, P], F32, tag="agg", name="agg_t")
             for t in range(PACK):
                 f_cols = slice(P * t, P * (t + 1))
                 for g in range(NODE_PASSES):
@@ -189,117 +234,205 @@ def tile_simplegcn_pa_kernel(tc, x, adj, W1, b1, out):
                         out=agg_t[:, t, :],
                         lhsT=x_codes[:, g, f_cols].bitcast(FP8X4),
                         lhsT_scale=x_scales[:, g, f_cols],
-                        rhs=n_codes[:, g, :].bitcast(FP8X4),
-                        rhs_scale=n_scales[:, g, :],
+                        rhs=codes[:, g, :].bitcast(FP8X4),
+                        rhs_scale=scales[:, g, :],
                         start=(g == 0),
                         stop=(g == NODE_PASSES - 1),
                     )
-            a_grouped = rows.tile([P, P, PACK], BF16, align_bytes=64, name="a_grouped")
-            nc.scalar.copy(out=a_grouped[:], in_=agg_t[:].rearrange("p t i -> p i t"))
-            return a_grouped
+            a_grouped[r] = rows.tile([P, P, PACK], BF16, align_bytes=64, name="a_grouped")
+            nc.scalar.copy(out=a_grouped[r][:], in_=agg_t[:].rearrange("p t i -> p i t"))
 
-        def quantise_agg(a_grouped):
+        def quantise_agg(r):
             a_codes = rows.tile([P, P], U32, align_bytes=64, name="a_codes")
             a_scales = rows.tile([P, P], U8, align_bytes=64, name="a_scales")
             nc.vector.quantize_mx(
                 out=a_codes[:].bitcast(FP8X4),
                 scales=a_scales[:],
-                in_=a_grouped[:].rearrange("p i t -> p (i t)"),
+                in_=a_grouped[r][:].rearrange("p i t -> p (i t)"),
             )
-            return a_codes, a_scales
+            a_mx[r] = (a_codes, a_scales)
 
-        def hidden_direct(a_codes, a_scales):
-            o_sb = outs.tile([P, F_HID], F32, name="o_sb")
-            acc = psum_out.tile([P, N_MAX], F32, name="acc")
-            nc.tensor.matmul_mx(
-                out=acc[:],
-                lhsT=a_codes[:].bitcast(FP8X4),
-                lhsT_scale=a_scales[:],
-                rhs=w_codes[:, 0:N_MAX].bitcast(FP8X4),
-                rhs_scale=w_scales[:, 0:N_MAX],
-                start=True,
-                stop=True,
-            )
-            nc.vector.tensor_tensor(
-                out=o_sb[:, 0:N_MAX], in0=acc[:], in1=bias_sb[:, 0:N_MAX], op=ALU.add
-            )
-            return o_sb
+        acc_t, o_t, back = {}, {}, {}
+        b_col = keep.tile([P, PACK], F32)
 
-        def hidden_turned(a_codes, a_scales):
-            acc_t = psum_out.tile([P, PACK, P], F32, name="acc_t")
-            for c in range(PACK):
-                h_cols = slice(N_MAX + P * c, N_MAX + P * (c + 1))
+        def turn_bias():
+            b_t = psum_t.tile([P, PACK, P], BF16, tag="bank", name="b_t")
+            for c in range(TC):
+                nc.tensor.transpose(b_t[:, c, :], bias_sb[:, DIRECT + P * c : DIRECT + P * (c + 1)], ident_bf16[:])
+            nc.vector.tensor_copy(out=b_col[:, 0:TC], in_=b_t[:, 0:TC, 0])
+
+        def direct_parts():
+            res = []
+            c = 0
+            while c < DIRECT:
+                n = 512 if DIRECT - c >= 512 else 256 if DIRECT - c >= 256 else 128
+                res.append((c, n))
+                c += n
+            return res
+
+        def hidden(r):
+            accs[r] = []
+            for c, n in direct_parts():
+                acc = psum_out.tile([P, N_MAX], F32, tag="acc", name="acc")
+                cols = slice(c, c + n)
                 nc.tensor.matmul_mx(
-                    out=acc_t[:, c, :],
-                    lhsT=w_codes[:, h_cols].bitcast(FP8X4),
-                    lhsT_scale=w_scales[:, h_cols],
-                    rhs=a_codes[:].bitcast(FP8X4),
-                    rhs_scale=a_scales[:],
+                    out=acc[:, 0:n],
+                    lhsT=a_mx[r][0][:].bitcast(FP8X4),
+                    lhsT_scale=a_mx[r][1][:],
+                    rhs=w_codes[:, cols].bitcast(FP8X4),
+                    rhs_scale=w_scales[:, cols],
                     start=True,
                     stop=True,
                 )
-            o_t = rows.tile([P, PACK, P], F32, name="o_t")
-            for c in range(PACK):
+                accs[r].append(acc)
+            if TC:
+                acc_t[r] = psum_side.tile([P, TC, P], F32, tag="acc_t", name="acc_t")
+                for c in range(TC):
+                    cols = slice(DIRECT + P * c, DIRECT + P * (c + 1))
+                    nc.tensor.matmul_mx(
+                        out=acc_t[r][:, c, :],
+                        lhsT=w_codes[:, cols].bitcast(FP8X4),
+                        lhsT_scale=w_scales[:, cols],
+                        rhs=a_mx[r][0][:].bitcast(FP8X4),
+                        rhs_scale=a_mx[r][1][:],
+                        start=True,
+                        stop=True,
+                    )
+
+        def relu_turned(r):
+            o_t[r] = rows.tile([P, TC, P], F32, name="o_t")
+            for c in range(TC):
                 nc.scalar.activation(
-                    out=o_t[:, c, :], in_=acc_t[:, c, :], func=ACT.Relu, bias=b_col[:, c : c + 1]
+                    out=o_t[r][:, c, :], in_=acc_t[r][:, c, :], func=ACT.Relu, bias=b_col[:, c : c + 1]
                 )
-            return o_t
 
-        def turn_back(o_t):
-            back = psum_out.tile([P, PACK, P], F32, tag="back", name="back")
-            for c in range(PACK):
-                nc.tensor.transpose(back[:, c, :], o_t[:, c, :], ident_f32[:])
-            return back
+        def turn_back(r):
+            back[r] = psum_side.tile([P, TC, P], F32, tag="back", name="back")
+            for c in range(TC):
+                nc.tensor.transpose(back[r][:, c, :], o_t[r][:, c, :], ident_f32[:])
 
-        def finish_direct(r, o_sb):
-            nc.scalar.activation(out=o_sb[:, 0:N_MAX], in_=o_sb[:, 0:N_MAX], func=ACT.Relu)
-            nc.sync.dma_start(out=out[P * r : P * (r + 1), 0:N_MAX], in_=o_sb[:, 0:N_MAX])
+        def add_bias(r, h):
+            if h == 0:
+                o_sb[r] = io.tile([P, F_HID], F32, tag="io", name="o_sb")
+            parts = direct_parts()
+            if h < len(parts):
+                c, n = parts[h]
+                cols = slice(c, c + n)
+                nc.vector.tensor_tensor(out=o_sb[r][:, cols], in0=accs[r][h][:, 0:n], in1=bias_sb[:, cols], op=ALU.add)
 
-        def finish_turned(r, o_sb, back):
-            nc.scalar.copy(out=o_sb[:, N_MAX:F_HID], in_=back[:].rearrange("p c h -> p (c h)"))
-            nc.sync.dma_start(out=out[P * r : P * (r + 1), N_MAX:F_HID], in_=o_sb[:, N_MAX:F_HID])
+        def finish(r):
+            if DIRECT:
+                cols = slice(0, DIRECT)
+                nc.scalar.activation(out=o_sb[r][:, cols], in_=o_sb[r][:, cols], func=ACT.Relu)
 
-        def is_row_tile(r):
-            return 0 <= r < ROW_TILES
+        def finish_back(r):
+            if TC:
+                nc.scalar.copy(out=o_sb[r][:, DIRECT:F_HID], in_=back[r][:].rearrange("p c h -> p (c h)"))
+            nc.sync.dma_start(out=out[P * r : P * (r + 1), :], in_=o_sb[r][:])
 
-        scaled = {}
-        banks = {}
-        n_grouped = {}
-        n_mx = {}
-        a_grouped = {}
-        a_mx = {}
-        o_sb = {}
-        o_t = {}
-        back = {}
-        b_col = keep.tile([P, PACK], F32)
-        for r in range(AHEAD - 1):
-            scaled[r] = prescale(r)
-        with tc.manual_schedule():
-            b_t = psum_out.tile([P, PACK, P], BF16, tag="back", name="b_t")
-            for c in range(PACK):
-                nc.tensor.transpose(
-                    b_t[:, c, :], bias_sb[:, N_MAX + P * c : N_MAX + P * (c + 1)], ident_bf16[:]
-                )
-            nc.vector.tensor_copy(out=b_col[:], in_=b_t[:, :, 0])
-            pipeline_steps = range(-1, ROW_TILES + 3)
-            for k in pipeline_steps:
-                if is_row_tile(k):
-                    n_grouped[k] = scale_columns(banks[k])
-                if is_row_tile(k - 1):
-                    a_grouped[k - 1] = aggregate(n_mx[k - 1][0], n_mx[k - 1][1])
-                if is_row_tile(k - 2):
-                    o_sb[k - 2] = hidden_direct(a_mx[k - 2][0], a_mx[k - 2][1])
-                    o_t[k - 2] = hidden_turned(a_mx[k - 2][0], a_mx[k - 2][1])
-                if is_row_tile(k - 3):
-                    finish_direct(k - 3, o_sb[k - 3])
-                    back[k - 3] = turn_back(o_t[k - 3])
-                if is_row_tile(k + 1):
-                    banks[k + 1] = transpose_row_tile(scaled[k + 1])
-                if is_row_tile(k - 3):
-                    finish_turned(k - 3, o_sb[k - 3], back[k - 3])
-                if is_row_tile(k + AHEAD):
-                    scaled[k + AHEAD] = prescale(k + AHEAD)
-                if is_row_tile(k):
-                    n_mx[k] = quantise_n(n_grouped[k])
-                if is_row_tile(k - 1):
-                    a_mx[k - 1] = quantise_agg(a_grouped[k - 1])
+        part = {}
+        xg = {}
+        last_r = ROW_TILES - 1
+
+        def ok(r):
+            return 0 <= r <= last_r
+
+        def sums(w, ts):
+            if w not in part and "P" in SUMS[w]:
+                part[w] = psum_agg.tile([P, PACK, P], F32, tag="agg", name="part")
+            for t in ts:
+                rowsum(PACK * w + t, part.get(w))
+
+        sums(0, (0, 1, 2, 3))
+        factor(0)
+        sums(1, (0, 1))
+        spread(0)
+        for r in range(4):
+            normalise(r, 0, 1)
+        sums(1, (2, 3))
+        reduce_parts(1, part.get(1))
+        factor(1)
+        spread(1)
+        xg[0] = group_x(0)
+        xg[1] = group_x(1)
+        sums(2, (0, 1))
+        for r in range(4):
+            normalise(r, 1, 2)
+        quantise_x(0, xg[0])
+        for r in range(4, 6):
+            normalise(r, 0, 2)
+        quantise_x(1, xg[1])
+        sums(2, (2, 3))
+        reduce_parts(2, part.get(2))
+        factor(2)
+        spread(2)
+        for r in range(6, 8):
+            normalise(r, 0, 2)
+        sums(3, (0, 1))
+        for r in range(0, 4):
+            normalise(r, 2, 3)
+        sums(3, (2, 3))
+        reduce_parts(3, part.get(3))
+        factor(3)
+        spread(3)
+        for g in range(2, 4):
+            xg[g] = group_x(g)
+        for hb in range(HID_BLOCKS):
+            turn_w(hb)
+        for r in range(4, 6):
+            normalise(r, 2, 3)
+        normalise(0, 3, 4)
+        quantise_x(2, xg[2])
+        normalise(1, 3, 4)
+        turn(0)
+        quantise_x(3, xg[3])
+        normalise(2, 3, 4)
+        turn(1)
+        quantise_n(0)
+
+        queue = [(3, 3), (4, 3), (5, 3), (6, 2), (6, 3), (7, 2), (7, 3)]
+        queue += [(r, g) for r in range(8, ROW_TILES) for g in range(NODE_PASSES)]
+
+        def take(n):
+            runs = []
+            for i in range(n):
+                if not queue:
+                    break
+                r, g = queue.pop(0)
+                if runs and runs[-1][0] == r:
+                    runs[-1][2] = g + 1
+                else:
+                    runs.append([r, g, g + 1])
+            return runs
+
+        if TC:
+            turn_bias()
+        for k in range(0, ROW_TILES + 2):
+            runs = take(PER_STEP)
+            if ok(k - 2) and TC:
+                relu_turned(k - 2)
+            if ok(k):
+                aggregate(k)
+            if ok(k - 1):
+                quantise_agg(k - 1)
+            if ok(k - 2):
+                add_bias(k - 2, 0)
+            for r, lo, hi in runs[:1]:
+                normalise(r, lo, hi)
+            if ok(k - 2):
+                add_bias(k - 2, 1)
+                finish(k - 2)
+            for r, lo, hi in runs[1:]:
+                normalise(r, lo, hi)
+            if ok(k + 2):
+                turn(k + 2)
+            if ok(k - 2) and TC:
+                turn_back(k - 2)
+            if ok(k - 2):
+                finish_back(k - 2)
+            if k == 0:
+                quantise_w()
+            if ok(k - 1):
+                hidden(k - 1)
+            if ok(k + 1):
+                quantise_n(k + 1)

@@ -23,12 +23,14 @@ ROW_TILES = NODES // P
 NODE_PASSES = NODES // K_PASS
 HID_BLOCKS = F_HID // P
 N_MAX = 512
-LOADS = ("a0", "a1", "x0", "x1", "a2", "a3", "x2", "x3", "w0", "w1")
-PER_STEP = 3
-TC = 2
-DIRECT = F_HID - P * TC
-SUMS = ("VVVV", "VVPP", "PPSP", "PPSP")
-X_ENG = 'SVSV'
+LOADS = ("a0", "a1", "x0", "x1", "a2", "x2", "x3", "a3", "b0", "w0", "w1")
+STEPS = 12
+ET = ((), (0, 1, 2, 3), (4, 5, 6, 7))
+FILL = (8,)
+TURNED = (True, True, True, True, True, True, True, True, False, False, False, False, False, False, False, False)
+V_RELU = 99
+SUMS = ("VVVV", "VVPP", "PPPP", "PSPP")
+X_ENG = 'SSSV'
 DROW = "S"
 
 FLOPS = 2 * NODES * NODES * F_IN + 2 * NODES * F_IN * F_HID
@@ -41,7 +43,8 @@ def tile_simplegcn_pa_kernel(tc, x, adj, W1, b1, out):
         io = ctx.enter_context(tc.tile_pool(name="io", bufs=6))
         stage = ctx.enter_context(tc.tile_pool(name="stage", bufs=4))
         rows = ctx.enter_context(tc.tile_pool(name="rows", bufs=3))
-        psum_t = ctx.enter_context(tc.psum_pool(name="psum_t", bufs=3))
+        wide = ctx.enter_context(tc.tile_pool(name="wide", bufs=10))
+        psum_t = ctx.enter_context(tc.psum_pool(name="psum_t", bufs=4))
         psum_agg = ctx.enter_context(tc.psum_pool(name="psum_agg", bufs=1))
         psum_side = ctx.enter_context(tc.psum_pool(name="psum_side", bufs=1))
         psum_out = ctx.enter_context(tc.psum_pool(name="psum_out", bufs=2))
@@ -65,10 +68,13 @@ def tile_simplegcn_pa_kernel(tc, x, adj, W1, b1, out):
             for r in range(PACK * w, PACK * (w + 1)):
                 nc.sync.dma_start(out=adj_sb[:, r, :], in_=adj[P * r : P * (r + 1), :])
 
-        for item in LOADS:
-            {"x": load_x, "w": load_w, "a": load_adj}[item[0]](int(item[1]))
         bias_sb = keep.tile([P, F_HID], BF16)
-        nc.sync.dma_start(out=bias_sb[:], in_=b1.partition_broadcast(P))
+
+        def load_b(i):
+            nc.sync.dma_start(out=bias_sb[:], in_=b1.partition_broadcast(P))
+
+        for item in LOADS:
+            {"x": load_x, "w": load_w, "a": load_adj, "b": load_b}[item[0]](int(item[1]))
 
         ident_f32 = keep.tile([P, P], F32)
         make_identity(nc, ident_f32[:])
@@ -77,7 +83,7 @@ def tile_simplegcn_pa_kernel(tc, x, adj, W1, b1, out):
         eps_col = keep.tile([P, 1], F32)
         nc.vector.memset(eps_col[:], EPS)
         table_warm = keep.tile([P, 1], F32)
-        nc.scalar.activation(out=table_warm[:], in_=eps_col[:], func=ACT.Sqrt)
+        nc.scalar.activation(out=table_warm[:], in_=eps_col[:], func=ACT.Abs_reciprocal_sqrt)
 
         x_codes = keep.tile([P, NODE_PASSES, F_IN], U32, align_bytes=64)
         x_scales = keep.tile([P, NODE_PASSES, F_IN], U8, align_bytes=64)
@@ -125,7 +131,6 @@ def tile_simplegcn_pa_kernel(tc, x, adj, W1, b1, out):
             )
 
         deg = keep.tile([P, ROW_TILES], F32)
-        root = keep.tile([P, ROW_TILES], F32)
         d_col = keep.tile([P, ROW_TILES], F32)
         d_row = keep.tile([P, NODES], F32)
         unused_s = keep.tile([P, NODES], BF16)
@@ -160,31 +165,31 @@ def tile_simplegcn_pa_kernel(tc, x, adj, W1, b1, out):
         def reduce_parts(w, part):
             for t in range(PACK):
                 if SUMS[w][t] == "P":
-                    nc.vector.tensor_reduce(
-                        out=deg[:, PACK * w + t : PACK * w + t + 1], in_=part[:, t, :], axis=AXL.X, op=ALU.add
+                    nc.scalar.activation(
+                        out=unused_s[:, 0:P],
+                        in_=part[:, t, :],
+                        func=ACT.Copy,
+                        accum_out=deg[:, PACK * w + t : PACK * w + t + 1],
                     )
 
-        def factor(w):
+        def factors(w):
             cols = slice(PACK * w, PACK * (w + 1))
-            nc.scalar.activation(out=root[:, cols], in_=deg[:, cols], func=ACT.Sqrt, bias=eps_col[:, 0:1])
-            nc.vector.reciprocal(out=d_col[:, cols], in_=root[:, cols])
-
-        def spread(w):
             bank = psum_t.tile([P, PACK, P], F32, tag="bank", name="bank")
             for t in range(PACK):
                 r = PACK * w + t
-                nc.tensor.transpose(
-                    bank[:, t, :], d_col[:, r : r + 1].to_broadcast([P, P]), ident_f32[:]
-                )
-            dst = d_row[:, K_PASS * w : K_PASS * (w + 1)]
-            src = bank[:].rearrange("p t n -> p (t n)")
-            if DROW == "S":
-                nc.scalar.copy(out=dst, in_=src)
-            else:
-                nc.vector.tensor_copy(out=dst, in_=src)
+                nc.tensor.transpose(bank[:, t, :], deg[:, r : r + 1].to_broadcast([P, P]), ident_f32[:])
+            nc.scalar.activation(out=d_col[:, cols], in_=deg[:, cols], func=ACT.Abs_reciprocal_sqrt, bias=eps_col[:, 0:1])
+            nc.scalar.activation(
+                out=d_row[:, K_PASS * w : K_PASS * (w + 1)],
+                in_=bank[:].rearrange("p t n -> p (t n)"),
+                func=ACT.Abs_reciprocal_sqrt,
+                bias=eps_col[:, 0:1],
+            )
 
-        def normalise(r, w0, w1):
-            cols = slice(K_PASS * w0, K_PASS * w1)
+        scaled_to = [0] * ROW_TILES
+
+        def normalise(r, w1):
+            cols = slice(K_PASS * scaled_to[r], K_PASS * w1)
             nc.vector.scalar_tensor_tensor(
                 out=adj_sb[:, r, cols],
                 in0=adj_sb[:, r, cols],
@@ -193,12 +198,16 @@ def tile_simplegcn_pa_kernel(tc, x, adj, W1, b1, out):
                 op0=ALU.mult,
                 op1=ALU.mult,
             )
+            scaled_to[r] = w1
 
         n_grouped, n_mx, a_grouped, a_mx, accs, o_sb = {}, {}, {}, {}, {}, {}
 
+        turned_halves = set()
+
         def turn_half(r, h):
+            turned_halves.add((r, h))
             if r not in n_grouped:
-                n_grouped[r] = rows.tile([P, NODE_PASSES, P, PACK], BF16, align_bytes=64, name="n_grouped")
+                n_grouped[r] = wide.tile([P, NODE_PASSES, P, PACK], BF16, align_bytes=64, name="n_grouped")
             words = adj_sb[:, r, :].bitcast(F32)
             bank = psum_t.tile([P, PACK, P], F32, tag="bank", name="bank")
             for q in range(PACK):
@@ -211,8 +220,9 @@ def tile_simplegcn_pa_kernel(tc, x, adj, W1, b1, out):
             )
 
         def turn(r):
-            turn_half(r, 0)
-            turn_half(r, 1)
+            for h in range(2):
+                if (r, h) not in turned_halves:
+                    turn_half(r, h)
 
         def quantise_n(r):
             codes = rows.tile([P, NODE_PASSES, P], U32, align_bytes=64, name="n_codes")
@@ -257,38 +267,33 @@ def tile_simplegcn_pa_kernel(tc, x, adj, W1, b1, out):
 
         def turn_bias():
             b_t = psum_t.tile([P, PACK, P], BF16, tag="bank", name="b_t")
-            for c in range(TC):
-                nc.tensor.transpose(b_t[:, c, :], bias_sb[:, DIRECT + P * c : DIRECT + P * (c + 1)], ident_bf16[:])
-            nc.vector.tensor_copy(out=b_col[:, 0:TC], in_=b_t[:, 0:TC, 0])
+            for c in range(PACK):
+                nc.tensor.transpose(b_t[:, c, :], bias_sb[:, N_MAX + P * c : N_MAX + P * (c + 1)], ident_bf16[:])
+            nc.scalar.copy(out=b_col[:], in_=b_t[:, :, 0])
 
-        def direct_parts():
-            res = []
-            c = 0
-            while c < DIRECT:
-                n = 512 if DIRECT - c >= 512 else 256 if DIRECT - c >= 256 else 128
-                res.append((c, n))
-                c += n
-            return res
+        def direct_pass(r, c, n):
+            acc = psum_out.tile([P, N_MAX], F32, tag="acc", name="acc")
+            cols = slice(c, c + n)
+            nc.tensor.matmul_mx(
+                out=acc[:, 0:n],
+                lhsT=a_mx[r][0][:].bitcast(FP8X4),
+                lhsT_scale=a_mx[r][1][:],
+                rhs=w_codes[:, cols].bitcast(FP8X4),
+                rhs_scale=w_scales[:, cols],
+                start=True,
+                stop=True,
+            )
+            accs[r].append(acc)
 
         def hidden(r):
             accs[r] = []
-            for c, n in direct_parts():
-                acc = psum_out.tile([P, N_MAX], F32, tag="acc", name="acc")
-                cols = slice(c, c + n)
-                nc.tensor.matmul_mx(
-                    out=acc[:, 0:n],
-                    lhsT=a_mx[r][0][:].bitcast(FP8X4),
-                    lhsT_scale=a_mx[r][1][:],
-                    rhs=w_codes[:, cols].bitcast(FP8X4),
-                    rhs_scale=w_scales[:, cols],
-                    start=True,
-                    stop=True,
-                )
-                accs[r].append(acc)
-            if TC:
-                acc_t[r] = psum_side.tile([P, TC, P], F32, tag="acc_t", name="acc_t")
-                for c in range(TC):
-                    cols = slice(DIRECT + P * c, DIRECT + P * (c + 1))
+            direct_pass(r, 0, N_MAX)
+            if not TURNED[r]:
+                direct_pass(r, N_MAX, N_MAX)
+            else:
+                acc_t[r] = psum_out.tile([P, PACK, P], F32, tag="acc", name="acc_t")
+                for c in range(PACK):
+                    cols = slice(N_MAX + P * c, N_MAX + P * (c + 1))
                     nc.tensor.matmul_mx(
                         out=acc_t[r][:, c, :],
                         lhsT=w_codes[:, cols].bitcast(FP8X4),
@@ -300,35 +305,38 @@ def tile_simplegcn_pa_kernel(tc, x, adj, W1, b1, out):
                     )
 
         def relu_turned(r):
-            o_t[r] = rows.tile([P, TC, P], F32, name="o_t")
-            for c in range(TC):
-                nc.scalar.activation(
-                    out=o_t[r][:, c, :], in_=acc_t[r][:, c, :], func=ACT.Relu, bias=b_col[:, c : c + 1]
-                )
+            if TURNED[r]:
+                o_t[r] = rows.tile([P, PACK, P], F32, name="o_t")
+                for c in range(PACK):
+                    nc.scalar.activation(
+                        out=o_t[r][:, c, :], in_=acc_t[r][:, c, :], func=ACT.Relu, bias=b_col[:, c : c + 1]
+                    )
 
         def turn_back(r):
-            back[r] = psum_side.tile([P, TC, P], F32, tag="back", name="back")
-            for c in range(TC):
-                nc.tensor.transpose(back[r][:, c, :], o_t[r][:, c, :], ident_f32[:])
+            if TURNED[r]:
+                back[r] = psum_side.tile([P, PACK, P], F32, tag="back", name="back")
+                for c in range(PACK):
+                    nc.tensor.transpose(back[r][:, c, :], o_t[r][:, c, :], ident_f32[:])
 
         def add_bias(r, h):
             if h == 0:
                 o_sb[r] = io.tile([P, F_HID], F32, tag="io", name="o_sb")
-            parts = direct_parts()
-            if h < len(parts):
-                c, n = parts[h]
-                cols = slice(c, c + n)
-                nc.vector.tensor_tensor(out=o_sb[r][:, cols], in0=accs[r][h][:, 0:n], in1=bias_sb[:, cols], op=ALU.add)
+            if h == 0 or not TURNED[r]:
+                cols = slice(N_MAX * h, N_MAX * (h + 1))
+                nc.vector.tensor_tensor(out=o_sb[r][:, cols], in0=accs[r][h][:], in1=bias_sb[:, cols], op=ALU.add)
 
         def finish(r):
-            if DIRECT:
-                cols = slice(0, DIRECT)
-                nc.scalar.activation(out=o_sb[r][:, cols], in_=o_sb[r][:, cols], func=ACT.Relu)
+            n = N_MAX if TURNED[r] else F_HID
+            if r >= V_RELU:
+                nc.vector.tensor_scalar(out=o_sb[r][:, 0:n], in0=o_sb[r][:, 0:n], scalar1=0.0, scalar2=None, op0=ALU.max)
+            else:
+                nc.scalar.activation(out=o_sb[r][:, 0:n], in_=o_sb[r][:, 0:n], func=ACT.Relu)
+            nc.sync.dma_start(out=out[P * r : P * (r + 1), 0:n], in_=o_sb[r][:, 0:n])
 
         def finish_back(r):
-            if TC:
-                nc.scalar.copy(out=o_sb[r][:, DIRECT:F_HID], in_=back[r][:].rearrange("p c h -> p (c h)"))
-            nc.sync.dma_start(out=out[P * r : P * (r + 1), :], in_=o_sb[r][:])
+            if TURNED[r]:
+                nc.scalar.copy(out=o_sb[r][:, N_MAX:F_HID], in_=back[r][:].rearrange("p c h -> p (c h)"))
+                nc.sync.dma_start(out=out[P * r : P * (r + 1), N_MAX:F_HID], in_=o_sb[r][:, N_MAX:F_HID])
 
         part = {}
         xg = {}
@@ -344,54 +352,64 @@ def tile_simplegcn_pa_kernel(tc, x, adj, W1, b1, out):
                 rowsum(PACK * w + t, part.get(w))
 
         sums(0, (0, 1, 2, 3))
-        factor(0)
+        factors(0)
         sums(1, (0, 1))
-        spread(0)
         for r in range(4):
-            normalise(r, 0, 1)
+            normalise(r, 1)
         sums(1, (2, 3))
         reduce_parts(1, part.get(1))
-        factor(1)
-        spread(1)
+        factors(1)
         xg[0] = group_x(0)
         xg[1] = group_x(1)
         sums(2, (0, 1))
         for r in range(4):
-            normalise(r, 1, 2)
+            normalise(r, 2)
         quantise_x(0, xg[0])
         for r in range(4, 6):
-            normalise(r, 0, 2)
+            normalise(r, 2)
         quantise_x(1, xg[1])
+        for r in range(6, 8):
+            normalise(r, 2)
         sums(2, (2, 3))
         reduce_parts(2, part.get(2))
-        factor(2)
-        spread(2)
-        for r in range(6, 8):
-            normalise(r, 0, 2)
-        sums(3, (0, 1))
+        factors(2)
+        for r in ET[0]:
+            turn_half(r, 0)
+        xg[2] = group_x(2)
+        for r in ET[1]:
+            turn_half(r, 0)
+        xg[3] = group_x(3)
+        sums(3, (0, 1, 2))
         for r in range(0, 4):
-            normalise(r, 2, 3)
-        sums(3, (2, 3))
+            normalise(r, 3)
+        quantise_x(2, xg[2])
+        for r in range(4, 8):
+            normalise(r, 3)
+        quantise_x(3, xg[3])
+        sums(3, (3,))
         reduce_parts(3, part.get(3))
-        factor(3)
-        spread(3)
-        for g in range(2, 4):
-            xg[g] = group_x(g)
+        factors(3)
+        for r in ET[2]:
+            turn_half(r, 0)
+        for r in FILL:
+            normalise(r, 3)
+        normalise(0, 4)
+        normalise(1, 4)
+        turn(0)
+        normalise(2, 4)
+        turn(1)
         for hb in range(HID_BLOCKS):
             turn_w(hb)
-        for r in range(4, 6):
-            normalise(r, 2, 3)
-        normalise(0, 3, 4)
-        quantise_x(2, xg[2])
-        normalise(1, 3, 4)
-        turn(0)
-        quantise_x(3, xg[3])
-        normalise(2, 3, 4)
-        turn(1)
+        normalise(3, 4)
         quantise_n(0)
 
-        queue = [(3, 3), (4, 3), (5, 3), (6, 2), (6, 3), (7, 2), (7, 3)]
-        queue += [(r, g) for r in range(8, ROW_TILES) for g in range(NODE_PASSES)]
+        queue = [(r, g) for r in range(ROW_TILES) for g in range(scaled_to[r], NODE_PASSES)]
+
+        total = len(queue)
+
+        def budget(k):
+            want = -(-total * (k + 1) // STEPS)
+            return max(0, want - (total - len(queue)))
 
         def take(n):
             runs = []
@@ -400,16 +418,14 @@ def tile_simplegcn_pa_kernel(tc, x, adj, W1, b1, out):
                     break
                 r, g = queue.pop(0)
                 if runs and runs[-1][0] == r:
-                    runs[-1][2] = g + 1
+                    runs[-1][1] = g + 1
                 else:
-                    runs.append([r, g, g + 1])
+                    runs.append([r, g + 1])
             return runs
 
-        if TC:
-            turn_bias()
         for k in range(0, ROW_TILES + 2):
-            runs = take(PER_STEP)
-            if ok(k - 2) and TC:
+            runs = take(budget(k))
+            if ok(k - 2):
                 relu_turned(k - 2)
             if ok(k):
                 aggregate(k)
@@ -417,21 +433,21 @@ def tile_simplegcn_pa_kernel(tc, x, adj, W1, b1, out):
                 quantise_agg(k - 1)
             if ok(k - 2):
                 add_bias(k - 2, 0)
-            for r, lo, hi in runs[:1]:
-                normalise(r, lo, hi)
+            for r, hi in runs[:1]:
+                normalise(r, hi)
             if ok(k - 2):
                 add_bias(k - 2, 1)
                 finish(k - 2)
-            for r, lo, hi in runs[1:]:
-                normalise(r, lo, hi)
+            for r, hi in runs[1:]:
+                normalise(r, hi)
             if ok(k + 2):
                 turn(k + 2)
-            if ok(k - 2) and TC:
-                turn_back(k - 2)
             if ok(k - 2):
+                turn_back(k - 2)
                 finish_back(k - 2)
             if k == 0:
                 quantise_w()
+                turn_bias()
             if ok(k - 1):
                 hidden(k - 1)
             if ok(k + 1):

@@ -23,13 +23,16 @@ ROW_TILES = NODES // P
 NODE_PASSES = NODES // K_PASS
 HID_BLOCKS = F_HID // P
 N_MAX = 512
-LOADS = ("a0", "a1", "x0", "x1", "a2", "x2", "x3", "a3", "b0", "w0", "w1")
-STEPS = 12
-ET = ((), (0, 1, 2, 3), (4, 5, 6, 7))
-FILL = (8,)
-TURNED = (True, True, True, True, True, True, True, True, False, False, False, False, False, False, False, False)
-V_RELU = 99
-SUMS = ("VVVV", "VVPP", "PPPP", "PSPP")
+LOADS = ('a0', 'a1', 'x0', 'x1', 'a2', 'x2', 'x3', 'a3', 'b0', 'w0', 'w1')
+STEPS = 14
+ET = ((0, 1), (2, 3), (4, 5))
+FILL = ()
+F2 = (8, 9)
+XG = (3, 3, 4, 5)
+XQ = (2, 3, 4, 5)
+TB = (4, 4, 4, 4, 2, 2, 2, 2, 2, 2, 2, 2, 0, 0, 0, 0)
+V_RELU = 13
+SUMS = ('VVVV', 'VSPV', 'PPPP', 'PPPP')
 X_ENG = 'SSSV'
 DROW = "S"
 
@@ -271,11 +274,13 @@ def tile_simplegcn_pa_kernel(tc, x, adj, W1, b1, out):
                 nc.tensor.transpose(b_t[:, c, :], bias_sb[:, N_MAX + P * c : N_MAX + P * (c + 1)], ident_bf16[:])
             nc.scalar.copy(out=b_col[:], in_=b_t[:, :, 0])
 
-        def direct_pass(r, c, n):
-            acc = psum_out.tile([P, N_MAX], F32, tag="acc", name="acc")
-            cols = slice(c, c + n)
+        def direct_end(r):
+            return F_HID - P * TB[r]
+
+        def direct_pass(acc, r, c, done, n):
+            cols = slice(c + done, c + done + n)
             nc.tensor.matmul_mx(
-                out=acc[:, 0:n],
+                out=acc[:, done : done + n],
                 lhsT=a_mx[r][0][:].bitcast(FP8X4),
                 lhsT_scale=a_mx[r][1][:],
                 rhs=w_codes[:, cols].bitcast(FP8X4),
@@ -283,60 +288,79 @@ def tile_simplegcn_pa_kernel(tc, x, adj, W1, b1, out):
                 start=True,
                 stop=True,
             )
-            accs[r].append(acc)
 
         def hidden(r):
             accs[r] = []
-            direct_pass(r, 0, N_MAX)
-            if not TURNED[r]:
-                direct_pass(r, N_MAX, N_MAX)
-            else:
-                acc_t[r] = psum_out.tile([P, PACK, P], F32, tag="acc", name="acc_t")
-                for c in range(PACK):
-                    cols = slice(N_MAX + P * c, N_MAX + P * (c + 1))
-                    nc.tensor.matmul_mx(
-                        out=acc_t[r][:, c, :],
-                        lhsT=w_codes[:, cols].bitcast(FP8X4),
-                        lhsT_scale=w_scales[:, cols],
-                        rhs=a_mx[r][0][:].bitcast(FP8X4),
-                        rhs_scale=a_mx[r][1][:],
-                        start=True,
-                        stop=True,
-                    )
+            for h in range(2):
+                acc = psum_out.tile([P, N_MAX], F32, tag="acc", name="acc")
+                accs[r].append(acc)
+                n = min(N_MAX, direct_end(r) - N_MAX * h)
+                done = 0
+                for width in (512, 256, 128):
+                    if n - done >= width:
+                        direct_pass(acc, r, N_MAX * h, done, width)
+                        done += width
+            for c in range(PACK - TB[r], PACK):
+                cols = slice(N_MAX + P * c, N_MAX + P * (c + 1))
+                nc.tensor.matmul_mx(
+                    out=accs[r][1][:, P * c : P * (c + 1)],
+                    lhsT=w_codes[:, cols].bitcast(FP8X4),
+                    lhsT_scale=w_scales[:, cols],
+                    rhs=a_mx[r][0][:].bitcast(FP8X4),
+                    rhs_scale=a_mx[r][1][:],
+                    start=True,
+                    stop=True,
+                )
 
         def relu_turned(r):
-            if TURNED[r]:
+            if TB[r]:
                 o_t[r] = rows.tile([P, PACK, P], F32, name="o_t")
-                for c in range(PACK):
+                for c in range(PACK - TB[r], PACK):
                     nc.scalar.activation(
-                        out=o_t[r][:, c, :], in_=acc_t[r][:, c, :], func=ACT.Relu, bias=b_col[:, c : c + 1]
+                        out=o_t[r][:, c, :],
+                        in_=accs[r][1][:, P * c : P * (c + 1)],
+                        func=ACT.Relu,
+                        bias=b_col[:, c : c + 1],
                     )
 
         def turn_back(r):
-            if TURNED[r]:
+            if TB[r]:
                 back[r] = psum_side.tile([P, PACK, P], F32, tag="back", name="back")
-                for c in range(PACK):
+                for c in range(PACK - TB[r], PACK):
                     nc.tensor.transpose(back[r][:, c, :], o_t[r][:, c, :], ident_f32[:])
 
         def add_bias(r, h):
             if h == 0:
                 o_sb[r] = io.tile([P, F_HID], F32, tag="io", name="o_sb")
-            if h == 0 or not TURNED[r]:
-                cols = slice(N_MAX * h, N_MAX * (h + 1))
-                nc.vector.tensor_tensor(out=o_sb[r][:, cols], in0=accs[r][h][:], in1=bias_sb[:, cols], op=ALU.add)
+            n = min(N_MAX, direct_end(r) - N_MAX * h)
+            if n > 0:
+                cols = slice(N_MAX * h, N_MAX * h + n)
+                nc.vector.tensor_tensor(
+                    out=o_sb[r][:, cols], in0=accs[r][h][:, 0:n], in1=bias_sb[:, cols], op=ALU.add
+                )
 
         def finish(r):
-            n = N_MAX if TURNED[r] else F_HID
+            n = direct_end(r)
             if r >= V_RELU:
-                nc.vector.tensor_scalar(out=o_sb[r][:, 0:n], in0=o_sb[r][:, 0:n], scalar1=0.0, scalar2=None, op0=ALU.max)
-            else:
-                nc.scalar.activation(out=o_sb[r][:, 0:n], in_=o_sb[r][:, 0:n], func=ACT.Relu)
-            nc.sync.dma_start(out=out[P * r : P * (r + 1), 0:n], in_=o_sb[r][:, 0:n])
+                nc.scalar.activation(out=o_sb[r][:, 0:N_MAX], in_=o_sb[r][:, 0:N_MAX], func=ACT.Relu)
+                nc.sync.dma_start(out=out[P * r : P * (r + 1), 0:N_MAX], in_=o_sb[r][:, 0:N_MAX])
+                nc.vector.tensor_scalar(
+                    out=o_sb[r][:, N_MAX:F_HID], in0=o_sb[r][:, N_MAX:F_HID], scalar1=0.0, scalar2=None, op0=ALU.max
+                )
+                nc.sync.dma_start(out=out[P * r : P * (r + 1), N_MAX:F_HID], in_=o_sb[r][:, N_MAX:F_HID])
+                return
+            nc.scalar.activation(out=o_sb[r][:, 0:n], in_=o_sb[r][:, 0:n], func=ACT.Relu)
+            if not TB[r]:
+                nc.sync.dma_start(out=out[P * r : P * (r + 1), :], in_=o_sb[r][:])
 
         def finish_back(r):
-            if TURNED[r]:
-                nc.scalar.copy(out=o_sb[r][:, N_MAX:F_HID], in_=back[r][:].rearrange("p c h -> p (c h)"))
-                nc.sync.dma_start(out=out[P * r : P * (r + 1), N_MAX:F_HID], in_=o_sb[r][:, N_MAX:F_HID])
+            if TB[r]:
+                n = direct_end(r)
+                nc.scalar.copy(
+                    out=o_sb[r][:, n:F_HID],
+                    in_=back[r][:, PACK - TB[r] : PACK, :].rearrange("p c h -> p (c h)"),
+                )
+                nc.sync.dma_start(out=out[P * r : P * (r + 1), :], in_=o_sb[r][:])
 
         part = {}
         xg = {}
@@ -351,23 +375,37 @@ def tile_simplegcn_pa_kernel(tc, x, adj, W1, b1, out):
             for t in ts:
                 rowsum(PACK * w + t, part.get(w))
 
+        def groups(key):
+            for g in range(NODE_PASSES):
+                if XG[g] == key:
+                    xg[g] = group_x(g)
+
+        def quants(key):
+            for g in range(NODE_PASSES):
+                if XQ[g] == key:
+                    quantise_x(g, xg[g])
+
+        groups(0)
         sums(0, (0, 1, 2, 3))
+        groups(1)
+        quants(0)
         factors(0)
         sums(1, (0, 1))
+        groups(2)
         for r in range(4):
             normalise(r, 1)
         sums(1, (2, 3))
+        quants(1)
         reduce_parts(1, part.get(1))
         factors(1)
-        xg[0] = group_x(0)
-        xg[1] = group_x(1)
+        groups(3)
         sums(2, (0, 1))
         for r in range(4):
             normalise(r, 2)
-        quantise_x(0, xg[0])
+        quants(2)
         for r in range(4, 6):
             normalise(r, 2)
-        quantise_x(1, xg[1])
+        quants(3)
         for r in range(6, 8):
             normalise(r, 2)
         sums(2, (2, 3))
@@ -375,17 +413,17 @@ def tile_simplegcn_pa_kernel(tc, x, adj, W1, b1, out):
         factors(2)
         for r in ET[0]:
             turn_half(r, 0)
-        xg[2] = group_x(2)
+        groups(4)
         for r in ET[1]:
             turn_half(r, 0)
-        xg[3] = group_x(3)
+        groups(5)
         sums(3, (0, 1, 2))
         for r in range(0, 4):
             normalise(r, 3)
-        quantise_x(2, xg[2])
-        for r in range(4, 8):
+        quants(4)
+        for r in F2:
             normalise(r, 3)
-        quantise_x(3, xg[3])
+        quants(5)
         sums(3, (3,))
         reduce_parts(3, part.get(3))
         factors(3)
@@ -429,10 +467,10 @@ def tile_simplegcn_pa_kernel(tc, x, adj, W1, b1, out):
                 relu_turned(k - 2)
             if ok(k):
                 aggregate(k)
-            if ok(k - 1):
-                quantise_agg(k - 1)
             if ok(k - 2):
                 add_bias(k - 2, 0)
+            if ok(k - 1):
+                quantise_agg(k - 1)
             for r, hi in runs[:1]:
                 normalise(r, hi)
             if ok(k - 2):

@@ -23,17 +23,23 @@ ROW_TILES = NODES // P
 NODE_PASSES = NODES // K_PASS
 HID_BLOCKS = F_HID // P
 N_MAX = 512
-LOADS = ('a0', 'a1', 'x0', 'x1', 'a2', 'x2', 'x3', 'a3', 'b0', 'w0', 'w1')
+LOADS = ('b0', 'a0', 'x0', 'a1', 'x1', 'a2', 'x2', 'x3', 'a3', 'w0', 'w1')
 STEPS = 14
-ET = ((0, 1), (2, 3), (4, 5))
+ORDER = (('p', 0), ('A', 0), ('P', 0), ('R', -2), ('C', 0), ('T', 2), ('B', -2), ('K', -3), ('Q', -1), ('N', 1), ('w', 0), ('W', 2), ('b', -2), ('H', -1), ('k', -3), ('F', -2))
+HEADDONE = (('T', 0), ('T', 1), ('W', 0), ('W', 1), ('N', 0))
+FIRST = 0
+LAST = 3
+RS = 256
+ET = ((0, 1, 2), (3, 4, 5), (6, 7, 8))
 FILL = ()
-F2 = (8, 9)
-XG = (3, 3, 4, 5)
-XQ = (2, 3, 4, 5)
-TB = (4, 4, 4, 4, 2, 2, 2, 2, 2, 2, 2, 2, 0, 0, 0, 0)
-V_RELU = 13
+W2 = ((0, 1, 8), (9,), (10,))
+W1A = (0, 1, 2, 3)
+XG = (1, 3, 4, 5)
+XQ = (1, 3, 4, 5)
+TB = (0, 0, 0, 0, 0, 0, 0, 0, 0, 0, 0, 0, 0, 0, 0, 0)
+V_RELU = 14
 SUMS = ('VVVV', 'VSPV', 'PPPP', 'PPPP')
-X_ENG = 'SSSV'
+X_ENG = 'VSSV'
 DROW = "S"
 
 FLOPS = 2 * NODES * NODES * F_IN + 2 * NODES * F_IN * F_HID
@@ -50,7 +56,7 @@ def tile_simplegcn_pa_kernel(tc, x, adj, W1, b1, out):
         psum_t = ctx.enter_context(tc.psum_pool(name="psum_t", bufs=4))
         psum_agg = ctx.enter_context(tc.psum_pool(name="psum_agg", bufs=1))
         psum_side = ctx.enter_context(tc.psum_pool(name="psum_side", bufs=1))
-        psum_out = ctx.enter_context(tc.psum_pool(name="psum_out", bufs=2))
+        psum_out = ctx.enter_context(tc.psum_pool(name="psum_out", bufs=3))
         ctx.enter_context(tc.manual_schedule())
 
         x_view = x.rearrange("(g u p e) f -> p g u e f", p=P, u=2, e=2)
@@ -73,8 +79,20 @@ def tile_simplegcn_pa_kernel(tc, x, adj, W1, b1, out):
 
         bias_sb = keep.tile([P, F_HID], BF16)
 
+        bias_row = keep.tile([P, F_HID], BF16)
+        ones = keep.tile([P, P], BF16)
+        nc.vector.memset(bias_row[:], 0.0)
+        nc.vector.memset(ones[:], 1.0)
+
         def load_b(i):
-            nc.sync.dma_start(out=bias_sb[:], in_=b1.partition_broadcast(P))
+            nc.sync.dma_start(out=bias_row[0:1, :], in_=b1.unsqueeze(0))
+
+        def spread_bias():
+            for h in range(2):
+                cols = slice(N_MAX * h, N_MAX * (h + 1))
+                bank = psum_t.tile([P, N_MAX], F32, tag="bank", name="bank")
+                nc.tensor.matmul(bank[:], lhsT=ones[:], rhs=bias_row[:, cols], start=True, stop=True)
+                nc.scalar.copy(out=bias_sb[:, cols], in_=bank[:])
 
         for item in LOADS:
             {"x": load_x, "w": load_w, "a": load_adj, "b": load_b}[item[0]](int(item[1]))
@@ -156,24 +174,17 @@ def tile_simplegcn_pa_kernel(tc, x, adj, W1, b1, out):
                     accum_out=deg[:, r : r + 1],
                 )
             else:
-                for b in range(ROW_TILES):
+                for b in range(NODES // RS):
                     nc.tensor.matmul(
-                        part[:, r % PACK, :],
+                        part[:, :],
                         lhsT=ident_bf16[:],
-                        rhs=adj_sb[:, r, P * b : P * (b + 1)],
+                        rhs=adj_sb[:, r, RS * b : RS * (b + 1)],
                         start=(b == 0),
-                        stop=(b == ROW_TILES - 1),
+                        stop=(b == NODES // RS - 1),
                     )
-
-        def reduce_parts(w, part):
-            for t in range(PACK):
-                if SUMS[w][t] == "P":
-                    nc.scalar.activation(
-                        out=unused_s[:, 0:P],
-                        in_=part[:, t, :],
-                        func=ACT.Copy,
-                        accum_out=deg[:, PACK * w + t : PACK * w + t + 1],
-                    )
+                nc.scalar.activation(
+                    out=unused_s[:, 0:RS], in_=part[:, :], func=ACT.Copy, accum_out=deg[:, r : r + 1]
+                )
 
         def factors(w):
             cols = slice(PACK * w, PACK * (w + 1))
@@ -203,11 +214,14 @@ def tile_simplegcn_pa_kernel(tc, x, adj, W1, b1, out):
             )
             scaled_to[r] = w1
 
+        aggs, word_banks = {}, {}
         n_grouped, n_mx, a_grouped, a_mx, accs, o_sb = {}, {}, {}, {}, {}, {}
 
         turned_halves = set()
+        copied = set()
 
         def turn_half(r, h):
+            assert scaled_to[r] >= 2 * h + 2
             turned_halves.add((r, h))
             if r not in n_grouped:
                 n_grouped[r] = wide.tile([P, NODE_PASSES, P, PACK], BF16, align_bytes=64, name="n_grouped")
@@ -216,16 +230,30 @@ def tile_simplegcn_pa_kernel(tc, x, adj, W1, b1, out):
             for q in range(PACK):
                 b = PACK * h + q
                 nc.tensor.transpose(bank[:, q, :], words[:, P * b : P * (b + 1)], ident_f32[:])
+            word_banks[r, h] = bank
+
+        def copy_half(r, h):
+            bank = word_banks[r, h]
             dst = n_grouped[r][:, 2 * h : 2 * h + 2, :, :].rearrange("p g i t -> p (g i t)").bitcast(F32)
             nc.scalar.copy(
                 out=dst.rearrange("p (g i u) -> p g i u", g=2, u=2),
                 in_=bank[:].rearrange("p (g u) i -> p g i u", u=2),
             )
 
-        def turn(r):
+        def turn_mm(r):
             for h in range(2):
                 if (r, h) not in turned_halves:
                     turn_half(r, h)
+
+        def copy_words(r):
+            for h in range(2):
+                if (r, h) in word_banks and (r, h) not in copied:
+                    copy_half(r, h)
+                    copied.add((r, h))
+
+        def turn(r):
+            turn_mm(r)
+            copy_words(r)
 
         def quantise_n(r):
             codes = rows.tile([P, NODE_PASSES, P], U32, align_bytes=64, name="n_codes")
@@ -252,8 +280,11 @@ def tile_simplegcn_pa_kernel(tc, x, adj, W1, b1, out):
                         start=(g == 0),
                         stop=(g == NODE_PASSES - 1),
                     )
+            aggs[r] = agg_t
+
+        def copy_agg(r):
             a_grouped[r] = rows.tile([P, P, PACK], BF16, align_bytes=64, name="a_grouped")
-            nc.scalar.copy(out=a_grouped[r][:], in_=agg_t[:].rearrange("p t i -> p i t"))
+            nc.scalar.copy(out=a_grouped[r][:], in_=aggs[r][:].rearrange("p t i -> p i t"))
 
         def quantise_agg(r):
             a_codes = rows.tile([P, P], U32, align_bytes=64, name="a_codes")
@@ -292,18 +323,22 @@ def tile_simplegcn_pa_kernel(tc, x, adj, W1, b1, out):
         def hidden(r):
             accs[r] = []
             for h in range(2):
+                n = min(N_MAX, direct_end(r) - N_MAX * h)
+                if n <= 0:
+                    continue
                 acc = psum_out.tile([P, N_MAX], F32, tag="acc", name="acc")
                 accs[r].append(acc)
-                n = min(N_MAX, direct_end(r) - N_MAX * h)
                 done = 0
                 for width in (512, 256, 128):
                     if n - done >= width:
                         direct_pass(acc, r, N_MAX * h, done, width)
                         done += width
+            if TB[r]:
+                acc_t[r] = psum_out.tile([P, N_MAX], F32, tag="acc", name="acc_t")
             for c in range(PACK - TB[r], PACK):
                 cols = slice(N_MAX + P * c, N_MAX + P * (c + 1))
                 nc.tensor.matmul_mx(
-                    out=accs[r][1][:, P * c : P * (c + 1)],
+                    out=acc_t[r][:, P * c : P * (c + 1)],
                     lhsT=w_codes[:, cols].bitcast(FP8X4),
                     lhsT_scale=w_scales[:, cols],
                     rhs=a_mx[r][0][:].bitcast(FP8X4),
@@ -318,7 +353,7 @@ def tile_simplegcn_pa_kernel(tc, x, adj, W1, b1, out):
                 for c in range(PACK - TB[r], PACK):
                     nc.scalar.activation(
                         out=o_t[r][:, c, :],
-                        in_=accs[r][1][:, P * c : P * (c + 1)],
+                        in_=acc_t[r][:, P * c : P * (c + 1)],
                         func=ACT.Relu,
                         bias=b_col[:, c : c + 1],
                     )
@@ -356,13 +391,15 @@ def tile_simplegcn_pa_kernel(tc, x, adj, W1, b1, out):
         def finish_back(r):
             if TB[r]:
                 n = direct_end(r)
+                copy_back(r, n)
+
+        def copy_back(r, n):
                 nc.scalar.copy(
                     out=o_sb[r][:, n:F_HID],
                     in_=back[r][:, PACK - TB[r] : PACK, :].rearrange("p c h -> p (c h)"),
                 )
                 nc.sync.dma_start(out=out[P * r : P * (r + 1), :], in_=o_sb[r][:])
 
-        part = {}
         xg = {}
         last_r = ROW_TILES - 1
 
@@ -370,10 +407,11 @@ def tile_simplegcn_pa_kernel(tc, x, adj, W1, b1, out):
             return 0 <= r <= last_r
 
         def sums(w, ts):
-            if w not in part and "P" in SUMS[w]:
-                part[w] = psum_agg.tile([P, PACK, P], F32, tag="agg", name="part")
             for t in ts:
-                rowsum(PACK * w + t, part.get(w))
+                part = None
+                if SUMS[w][t] == "P":
+                    part = psum_out.tile([P, RS], F32, tag="acc", name="part")
+                rowsum(PACK * w + t, part)
 
         def groups(key):
             for g in range(NODE_PASSES):
@@ -385,6 +423,7 @@ def tile_simplegcn_pa_kernel(tc, x, adj, W1, b1, out):
                 if XQ[g] == key:
                     quantise_x(g, xg[g])
 
+        spread_bias()
         groups(0)
         sums(0, (0, 1, 2, 3))
         groups(1)
@@ -396,11 +435,10 @@ def tile_simplegcn_pa_kernel(tc, x, adj, W1, b1, out):
             normalise(r, 1)
         sums(1, (2, 3))
         quants(1)
-        reduce_parts(1, part.get(1))
         factors(1)
         groups(3)
         sums(2, (0, 1))
-        for r in range(4):
+        for r in W1A:
             normalise(r, 2)
         quants(2)
         for r in range(4, 6):
@@ -409,33 +447,38 @@ def tile_simplegcn_pa_kernel(tc, x, adj, W1, b1, out):
         for r in range(6, 8):
             normalise(r, 2)
         sums(2, (2, 3))
-        reduce_parts(2, part.get(2))
         factors(2)
         for r in ET[0]:
             turn_half(r, 0)
+            copy_words(r)
         groups(4)
         for r in ET[1]:
             turn_half(r, 0)
+            copy_words(r)
         groups(5)
         sums(3, (0, 1, 2))
-        for r in range(0, 4):
+        for r in W2[0]:
             normalise(r, 3)
         quants(4)
-        for r in F2:
+        for r in W2[1]:
             normalise(r, 3)
         quants(5)
+        for r in W2[2]:
+            normalise(r, 3)
         sums(3, (3,))
-        reduce_parts(3, part.get(3))
         factors(3)
         for r in ET[2]:
             turn_half(r, 0)
+            copy_words(r)
         for r in FILL:
             normalise(r, 3)
         normalise(0, 4)
+        quants(6)
         normalise(1, 4)
         turn(0)
         normalise(2, 4)
         turn(1)
+        quants(7)
         for hb in range(HID_BLOCKS):
             turn_w(hb)
         normalise(3, 4)
@@ -461,32 +504,35 @@ def tile_simplegcn_pa_kernel(tc, x, adj, W1, b1, out):
                     runs.append([r, g + 1])
             return runs
 
-        for k in range(0, ROW_TILES + 2):
-            runs = take(budget(k))
-            if ok(k - 2):
-                relu_turned(k - 2)
-            if ok(k):
-                aggregate(k)
-            if ok(k - 2):
-                add_bias(k - 2, 0)
-            if ok(k - 1):
-                quantise_agg(k - 1)
-            for r, hi in runs[:1]:
+        def step_pieces(k, which):
+            if which == 0:
+                runs_now.clear()
+                runs_now.extend(take(budget(k)))
+            for r, hi in runs_now[:1] if which == 0 else runs_now[1:]:
                 normalise(r, hi)
-            if ok(k - 2):
-                add_bias(k - 2, 1)
-                finish(k - 2)
-            for r, hi in runs[1:]:
-                normalise(r, hi)
-            if ok(k + 2):
-                turn(k + 2)
-            if ok(k - 2):
-                turn_back(k - 2)
-                finish_back(k - 2)
-            if k == 0:
-                quantise_w()
-                turn_bias()
-            if ok(k - 1):
-                hidden(k - 1)
-            if ok(k + 1):
-                quantise_n(k + 1)
+
+        runs_now = []
+        ops = {
+            "R": relu_turned,
+            "A": aggregate,
+            "C": copy_agg,
+            "Q": quantise_agg,
+            "B": lambda r: add_bias(r, 0),
+            "b": lambda r: add_bias(r, 1),
+            "F": finish,
+            "T": turn_mm,
+            "W": copy_words,
+            "K": turn_back,
+            "k": finish_back,
+            "H": hidden,
+            "N": quantise_n,
+        }
+        for k in range(FIRST, ROW_TILES + LAST):
+            for op, off in ORDER:
+                if op == "p" or op == "P":
+                    step_pieces(k, 0 if op == "p" else 1)
+                elif op == "w":
+                    if k == off:
+                        quantise_w()
+                elif ok(k + off) and (op, k + off) not in HEADDONE:
+                    ops[op](k + off)

@@ -23,23 +23,24 @@ ROW_TILES = NODES // P
 NODE_PASSES = NODES // K_PASS
 HID_BLOCKS = F_HID // P
 N_MAX = 512
-LOADS = ('b0', 'a0', 'x0', 'a1', 'x1', 'a2', 'x2', 'x3', 'a3', 'w0', 'w1')
+LOADS = ('b0', 'a0', 'a1', 'x0', 'a2', 'x1', 'x2', 'x3', 'a3', 'w0', 'w1')
 STEPS = 14
-ORDER = (('p', 0), ('A', 0), ('P', 0), ('R', -2), ('C', 0), ('T', 2), ('B', -2), ('K', -3), ('Q', -1), ('N', 1), ('w', 0), ('W', 2), ('b', -2), ('H', -1), ('k', -3), ('F', -2))
+ORDER = (('p', 0), ('B', -2), ('Q', -1), ('b', -2), ('A', 0), ('N', 1), ('T', 2), ('C', 0), ('H', -1), ('W', 2), ('w', 0), ('P', 0), ('F', -2))
 HEADDONE = (('T', 0), ('T', 1), ('W', 0), ('W', 1), ('N', 0))
 FIRST = 0
-LAST = 3
-RS = 256
-ET = ((0, 1, 2), (3, 4, 5), (6, 7, 8))
+LAST = 2
+EC = (4,)
+RS = 128
+ET = ((), (), (0, 1, 2, 3))
 FILL = ()
-W2 = ((0, 1, 8), (9,), (10,))
+W2 = ((0, 1, 8), (9, 10), (11,))
 W1A = (0, 1, 2, 3)
-XG = (1, 3, 4, 5)
-XQ = (1, 3, 4, 5)
+XG = (3, 4, 4, 5)
+XQ = (3, 4, 5, 5)
 TB = (0, 0, 0, 0, 0, 0, 0, 0, 0, 0, 0, 0, 0, 0, 0, 0)
-V_RELU = 14
-SUMS = ('VVVV', 'VSPV', 'PPPP', 'PPPP')
-X_ENG = 'VSSV'
+V_RELU = 13
+SUMS = ('VSVV', 'VPPV', 'PPSP', 'PPPP')
+X_ENG = 'VSSS'
 DROW = "S"
 
 FLOPS = 2 * NODES * NODES * F_IN + 2 * NODES * F_IN * F_HID
@@ -186,13 +187,21 @@ def tile_simplegcn_pa_kernel(tc, x, adj, W1, b1, out):
                     out=unused_s[:, 0:RS], in_=part[:, :], func=ACT.Copy, accum_out=deg[:, r : r + 1]
                 )
 
+        def factor_cols(lo, hi):
+            nc.scalar.activation(
+                out=d_col[:, lo:hi], in_=deg[:, lo:hi], func=ACT.Abs_reciprocal_sqrt, bias=eps_col[:, 0:1]
+            )
+
         def factors(w):
             cols = slice(PACK * w, PACK * (w + 1))
             bank = psum_t.tile([P, PACK, P], F32, tag="bank", name="bank")
             for t in range(PACK):
                 r = PACK * w + t
                 nc.tensor.transpose(bank[:, t, :], deg[:, r : r + 1].to_broadcast([P, P]), ident_f32[:])
-            nc.scalar.activation(out=d_col[:, cols], in_=deg[:, cols], func=ACT.Abs_reciprocal_sqrt, bias=eps_col[:, 0:1])
+            if w != 1 or not EC:
+                factor_cols(PACK * w, PACK * (w + 1))
+            else:
+                factor_cols(PACK * w + 2, PACK * (w + 1))
             nc.scalar.activation(
                 out=d_row[:, K_PASS * w : K_PASS * (w + 1)],
                 in_=bank[:].rearrange("p t n -> p (t n)"),
@@ -433,7 +442,11 @@ def tile_simplegcn_pa_kernel(tc, x, adj, W1, b1, out):
         groups(2)
         for r in range(4):
             normalise(r, 1)
+        if EC:
+            factor_cols(4, 6)
         sums(1, (2, 3))
+        for r in EC:
+            normalise(r, 1)
         quants(1)
         factors(1)
         groups(3)
@@ -470,8 +483,10 @@ def tile_simplegcn_pa_kernel(tc, x, adj, W1, b1, out):
         for r in ET[2]:
             turn_half(r, 0)
             copy_words(r)
+        groups(6)
         for r in FILL:
             normalise(r, 3)
+        quants(6)
         normalise(0, 4)
         quants(6)
         normalise(1, 4)
@@ -482,6 +497,7 @@ def tile_simplegcn_pa_kernel(tc, x, adj, W1, b1, out):
         for hb in range(HID_BLOCKS):
             turn_w(hb)
         normalise(3, 4)
+        quants(7)
         quantise_n(0)
 
         queue = [(r, g) for r in range(ROW_TILES) for g in range(scaled_to[r], NODE_PASSES)]

from contextlib import ExitStack

import concourse.mybir as mybir
from concourse.masks import make_identity

F32 = mybir.dt.float32
BF16 = mybir.dt.bfloat16
U32 = mybir.dt.uint32
U8 = mybir.dt.uint8
FP8X4 = mybir.dt.float8_e4m3fn_x4
ALU = mybir.AluOpType
ACT = mybir.ActivationFunctionType
AXL = mybir.AxisListType

P = 128
PACK = 4
K_PASS = P * PACK
NODES = 2048
F_IN = 512
F_HID = 1024
EPS = 1e-8
ROW_TILES = NODES // P
NODE_PASSES = NODES // K_PASS
HID_BLOCKS = F_HID // P
N_MAX = 512
LOADS = ('b0', 'a0', 'a1', 'x0', 'a2', 'x1', 'x2', 'x3', 'a3', 'w0', 'w1')
STEPS = 14
ORDER = (('p', 0), ('B', -2), ('Q', -1), ('b', -2), ('A', 0), ('N', 1), ('T', 2), ('C', 0), ('H', -1), ('W', 2), ('w', 0), ('P', 0), ('F', -2))
HEADDONE = (('T', 0), ('T', 1), ('W', 0), ('W', 1), ('N', 0))
FIRST = 0
LAST = 2
EC = (4,)
RS = 128
ET = ((), (), (0, 1, 2, 3))
FILL = ()
W2 = ((0, 1, 8), (9, 10), (11,))
W1A = (0, 1, 2, 3)
XG = (3, 4, 4, 5)
XQ = (3, 4, 5, 5)
TB = (0, 0, 0, 0, 0, 0, 0, 0, 0, 0, 0, 0, 0, 0, 0, 0)
V_RELU = 13
SUMS = ('VSVV', 'VPPV', 'PPSP', 'PPPP')
X_ENG = 'VSSS'
DROW = "S"

FLOPS = 2 * NODES * NODES * F_IN + 2 * NODES * F_IN * F_HID


def tile_simplegcn_pa_kernel(tc, x, adj, W1, b1, out):
    nc = tc.nc
    with ExitStack() as ctx:
        keep = ctx.enter_context(tc.tile_pool(name="keep", bufs=1))
        io = ctx.enter_context(tc.tile_pool(name="io", bufs=6))
        stage = ctx.enter_context(tc.tile_pool(name="stage", bufs=4))
        rows = ctx.enter_context(tc.tile_pool(name="rows", bufs=3))
        wide = ctx.enter_context(tc.tile_pool(name="wide", bufs=10))
        psum_t = ctx.enter_context(tc.psum_pool(name="psum_t", bufs=4))
        psum_agg = ctx.enter_context(tc.psum_pool(name="psum_agg", bufs=1))
        psum_side = ctx.enter_context(tc.psum_pool(name="psum_side", bufs=1))
        psum_out = ctx.enter_context(tc.psum_pool(name="psum_out", bufs=3))
        ctx.enter_context(tc.manual_schedule())

        x_view = x.rearrange("(g u p e) f -> p g u e f", p=P, u=2, e=2)
        w_view = W1.rearrange("(b p) f -> p b f", p=P)
        x_sb = {}
        w_sb = {}
        adj_sb = keep.tile([P, ROW_TILES, NODES], BF16)

        def load_x(g):
            x_sb[g] = io.tile([P, 2, 2, F_IN], BF16, tag="io", name="x_raw")
            nc.sync.dma_start(out=x_sb[g][:], in_=x_view[:, g, :, :, :])

        def load_w(h):
            w_sb[h] = io.tile([P, PACK, F_IN], BF16, tag="io", name="w_raw")
            nc.sync.dma_start(out=w_sb[h][:], in_=w_view[:, PACK * h : PACK * (h + 1), :])

        def load_adj(w):
            for r in range(PACK * w, PACK * (w + 1)):
                nc.sync.dma_start(out=adj_sb[:, r, :], in_=adj[P * r : P * (r + 1), :])

        bias_sb = keep.tile([P, F_HID], BF16)

        bias_row = keep.tile([P, F_HID], BF16)
        ones = keep.tile([P, P], BF16)
        nc.vector.memset(bias_row[:], 0.0)
        nc.vector.memset(ones[:], 1.0)

        def load_b(i):
            nc.sync.dma_start(out=bias_row[0:1, :], in_=b1.unsqueeze(0))

        def spread_bias():
            for h in range(2):
                cols = slice(N_MAX * h, N_MAX * (h + 1))
                bank = psum_t.tile([P, N_MAX], F32, tag="bank", name="bank")
                nc.tensor.matmul(bank[:], lhsT=ones[:], rhs=bias_row[:, cols], start=True, stop=True)
                nc.scalar.copy(out=bias_sb[:, cols], in_=bank[:])

        for item in LOADS:
            {"x": load_x, "w": load_w, "a": load_adj, "b": load_b}[item[0]](int(item[1]))

        ident_f32 = keep.tile([P, P], F32)
        make_identity(nc, ident_f32[:])
        ident_bf16 = keep.tile([P, P], BF16)
        make_identity(nc, ident_bf16[:])
        eps_col = keep.tile([P, 1], F32)
        nc.vector.memset(eps_col[:], EPS)
        table_warm = keep.tile([P, 1], F32)
        nc.scalar.activation(out=table_warm[:], in_=eps_col[:], func=ACT.Abs_reciprocal_sqrt)

        x_codes = keep.tile([P, NODE_PASSES, F_IN], U32, align_bytes=64)
        x_scales = keep.tile([P, NODE_PASSES, F_IN], U8, align_bytes=64)

        def group_x(g):
            x_grouped = stage.tile([P, F_IN, PACK], BF16, align_bytes=64, name="x_grouped")
            dst = x_grouped[:].rearrange("p (c i) t -> p c t i", i=4)
            src = x_sb[g][:].rearrange("p u e (c i) -> p c (u e) i", i=4)
            if X_ENG[g] == "S":
                nc.scalar.copy(out=dst, in_=src)
            elif X_ENG[g] == "V":
                nc.vector.tensor_copy(out=dst, in_=src)
            else:
                nc.gpsimd.tensor_scalar(
                    out=dst, in0=src, scalar1=1.0, scalar2=0.0, op0=ALU.mult, op1=ALU.add
                )
            return x_grouped

        def quantise_x(g, x_grouped):
            nc.vector.quantize_mx(
                out=x_codes[:, g, :].bitcast(FP8X4),
                scales=x_scales[:, g, :],
                in_=x_grouped[:].rearrange("p f t -> p (f t)"),
            )

        w_grouped = keep.tile([P, F_HID, PACK], BF16, align_bytes=64)
        w_codes = keep.tile([P, F_HID], U32, align_bytes=64)
        w_scales = keep.tile([P, F_HID], U8, align_bytes=64)

        def turn_w(hb):
            w_t = psum_t.tile([P, PACK, P], BF16, tag="bank", name="w_t")
            for t in range(PACK):
                nc.tensor.transpose(
                    w_t[:, t, :], w_sb[hb // PACK][:, hb % PACK, P * t : P * (t + 1)], ident_bf16[:]
                )
            nc.scalar.copy(
                out=w_grouped[:, P * hb : P * (hb + 1), :], in_=w_t[:].rearrange("p t h -> p h t")
            )

        def quantise_w():
            nc.vector.quantize_mx(
                out=w_codes[:].bitcast(FP8X4),
                scales=w_scales[:],
                in_=w_grouped[:].rearrange("p h t -> p (h t)"),
            )

        deg = keep.tile([P, ROW_TILES], F32)
        d_col = keep.tile([P, ROW_TILES], F32)
        d_row = keep.tile([P, NODES], F32)
        unused_s = keep.tile([P, NODES], BF16)
        unused_v = keep.tile([P, NODES], BF16)

        def rowsum(r, part):
            e = SUMS[r // PACK][r % PACK]
            if e == "S":
                nc.scalar.activation(
                    out=unused_s[:], in_=adj_sb[:, r, :], func=ACT.Copy, accum_out=deg[:, r : r + 1]
                )
            elif e == "V":
                nc.vector.tensor_scalar(
                    out=unused_v[:],
                    in0=adj_sb[:, r, :],
                    scalar1=1.0,
                    scalar2=None,
                    op0=ALU.mult,
                    op1=ALU.add,
                    accum_out=deg[:, r : r + 1],
                )
            else:
                for b in range(NODES // RS):
                    nc.tensor.matmul(
                        part[:, :],
                        lhsT=ident_bf16[:],
                        rhs=adj_sb[:, r, RS * b : RS * (b + 1)],
                        start=(b == 0),
                        stop=(b == NODES // RS - 1),
                    )
                nc.scalar.activation(
                    out=unused_s[:, 0:RS], in_=part[:, :], func=ACT.Copy, accum_out=deg[:, r : r + 1]
                )

        def factor_cols(lo, hi):
            nc.scalar.activation(
                out=d_col[:, lo:hi], in_=deg[:, lo:hi], func=ACT.Abs_reciprocal_sqrt, bias=eps_col[:, 0:1]
            )

        def factors(w):
            cols = slice(PACK * w, PACK * (w + 1))
            bank = psum_t.tile([P, PACK, P], F32, tag="bank", name="bank")
            for t in range(PACK):
                r = PACK * w + t
                nc.tensor.transpose(bank[:, t, :], deg[:, r : r + 1].to_broadcast([P, P]), ident_f32[:])
            if w != 1 or not EC:
                factor_cols(PACK * w, PACK * (w + 1))
            else:
                factor_cols(PACK * w + 2, PACK * (w + 1))
            nc.scalar.activation(
                out=d_row[:, K_PASS * w : K_PASS * (w + 1)],
                in_=bank[:].rearrange("p t n -> p (t n)"),
                func=ACT.Abs_reciprocal_sqrt,
                bias=eps_col[:, 0:1],
            )

        scaled_to = [0] * ROW_TILES

        def normalise(r, w1):
            cols = slice(K_PASS * scaled_to[r], K_PASS * w1)
            nc.vector.scalar_tensor_tensor(
                out=adj_sb[:, r, cols],
                in0=adj_sb[:, r, cols],
                scalar=d_col[:, r : r + 1],
                in1=d_row[:, cols],
                op0=ALU.mult,
                op1=ALU.mult,
            )
            scaled_to[r] = w1

        aggs, word_banks = {}, {}
        n_grouped, n_mx, a_grouped, a_mx, accs, o_sb = {}, {}, {}, {}, {}, {}

        turned_halves = set()
        copied = set()

        def turn_half(r, h):
            assert scaled_to[r] >= 2 * h + 2
            turned_halves.add((r, h))
            if r not in n_grouped:
                n_grouped[r] = wide.tile([P, NODE_PASSES, P, PACK], BF16, align_bytes=64, name="n_grouped")
            words = adj_sb[:, r, :].bitcast(F32)
            bank = psum_t.tile([P, PACK, P], F32, tag="bank", name="bank")
            for q in range(PACK):
                b = PACK * h + q
                nc.tensor.transpose(bank[:, q, :], words[:, P * b : P * (b + 1)], ident_f32[:])
            word_banks[r, h] = bank

        def copy_half(r, h):
            bank = word_banks[r, h]
            dst = n_grouped[r][:, 2 * h : 2 * h + 2, :, :].rearrange("p g i t -> p (g i t)").bitcast(F32)
            nc.scalar.copy(
                out=dst.rearrange("p (g i u) -> p g i u", g=2, u=2),
                in_=bank[:].rearrange("p (g u) i -> p g i u", u=2),
            )

        def turn_mm(r):
            for h in range(2):
                if (r, h) not in turned_halves:
                    turn_half(r, h)

        def copy_words(r):
            for h in range(2):
                if (r, h) in word_banks and (r, h) not in copied:
                    copy_half(r, h)
                    copied.add((r, h))

        def turn(r):
            turn_mm(r)
            copy_words(r)

        def quantise_n(r):
            codes = rows.tile([P, NODE_PASSES, P], U32, align_bytes=64, name="n_codes")
            scales = rows.tile([P, NODE_PASSES, P], U8, align_bytes=64, name="n_scales")
            nc.vector.quantize_mx(
                out=codes[:].rearrange("p g i -> p (g i)").bitcast(FP8X4),
                scales=scales[:].rearrange("p g i -> p (g i)"),
                in_=n_grouped[r][:].rearrange("p g i t -> p (g i t)"),
            )
            n_mx[r] = (codes, scales)

        def aggregate(r):
            codes, scales = n_mx[r]
            agg_t = psum_agg.tile([P, PACK, P], F32, tag="agg", name="agg_t")
            for t in range(PACK):
                f_cols = slice(P * t, P * (t + 1))
                for g in range(NODE_PASSES):
                    nc.tensor.matmul_mx(
                        out=agg_t[:, t, :],
                        lhsT=x_codes[:, g, f_cols].bitcast(FP8X4),
                        lhsT_scale=x_scales[:, g, f_cols],
                        rhs=codes[:, g, :].bitcast(FP8X4),
                        rhs_scale=scales[:, g, :],
                        start=(g == 0),
                        stop=(g == NODE_PASSES - 1),
                    )
            aggs[r] = agg_t

        def copy_agg(r):
            a_grouped[r] = rows.tile([P, P, PACK], BF16, align_bytes=64, name="a_grouped")
            nc.scalar.copy(out=a_grouped[r][:], in_=aggs[r][:].rearrange("p t i -> p i t"))

        def quantise_agg(r):
            a_codes = rows.tile([P, P], U32, align_bytes=64, name="a_codes")
            a_scales = rows.tile([P, P], U8, align_bytes=64, name="a_scales")
            nc.vector.quantize_mx(
                out=a_codes[:].bitcast(FP8X4),
                scales=a_scales[:],
                in_=a_grouped[r][:].rearrange("p i t -> p (i t)"),
            )
            a_mx[r] = (a_codes, a_scales)

        acc_t, o_t, back = {}, {}, {}
        b_col = keep.tile([P, PACK], F32)

        def turn_bias():
            b_t = psum_t.tile([P, PACK, P], BF16, tag="bank", name="b_t")
            for c in range(PACK):
                nc.tensor.transpose(b_t[:, c, :], bias_sb[:, N_MAX + P * c : N_MAX + P * (c + 1)], ident_bf16[:])
            nc.scalar.copy(out=b_col[:], in_=b_t[:, :, 0])

        def direct_end(r):
            return F_HID - P * TB[r]

        def direct_pass(acc, r, c, done, n):
            cols = slice(c + done, c + done + n)
            nc.tensor.matmul_mx(
                out=acc[:, done : done + n],
                lhsT=a_mx[r][0][:].bitcast(FP8X4),
                lhsT_scale=a_mx[r][1][:],
                rhs=w_codes[:, cols].bitcast(FP8X4),
                rhs_scale=w_scales[:, cols],
                start=True,
                stop=True,
            )

        def hidden(r):
            accs[r] = []
            for h in range(2):
                n = min(N_MAX, direct_end(r) - N_MAX * h)
                if n <= 0:
                    continue
                acc = psum_out.tile([P, N_MAX], F32, tag="acc", name="acc")
                accs[r].append(acc)
                done = 0
                for width in (512, 256, 128):
                    if n - done >= width:
                        direct_pass(acc, r, N_MAX * h, done, width)
                        done += width
            if TB[r]:
                acc_t[r] = psum_out.tile([P, N_MAX], F32, tag="acc", name="acc_t")
            for c in range(PACK - TB[r], PACK):
                cols = slice(N_MAX + P * c, N_MAX + P * (c + 1))
                nc.tensor.matmul_mx(
                    out=acc_t[r][:, P * c : P * (c + 1)],
                    lhsT=w_codes[:, cols].bitcast(FP8X4),
                    lhsT_scale=w_scales[:, cols],
                    rhs=a_mx[r][0][:].bitcast(FP8X4),
                    rhs_scale=a_mx[r][1][:],
                    start=True,
                    stop=True,
                )

        def relu_turned(r):
            if TB[r]:
                o_t[r] = rows.tile([P, PACK, P], F32, name="o_t")
                for c in range(PACK - TB[r], PACK):
                    nc.scalar.activation(
                        out=o_t[r][:, c, :],
                        in_=acc_t[r][:, P * c : P * (c + 1)],
                        func=ACT.Relu,
                        bias=b_col[:, c : c + 1],
                    )

        def turn_back(r):
            if TB[r]:
                back[r] = psum_side.tile([P, PACK, P], F32, tag="back", name="back")
                for c in range(PACK - TB[r], PACK):
                    nc.tensor.transpose(back[r][:, c, :], o_t[r][:, c, :], ident_f32[:])

        def add_bias(r, h):
            if h == 0:
                o_sb[r] = io.tile([P, F_HID], F32, tag="io", name="o_sb")
            n = min(N_MAX, direct_end(r) - N_MAX * h)
            if n > 0:
                cols = slice(N_MAX * h, N_MAX * h + n)
                nc.vector.tensor_tensor(
                    out=o_sb[r][:, cols], in0=accs[r][h][:, 0:n], in1=bias_sb[:, cols], op=ALU.add
                )

        def finish(r):
            n = direct_end(r)
            if r >= V_RELU:
                nc.scalar.activation(out=o_sb[r][:, 0:N_MAX], in_=o_sb[r][:, 0:N_MAX], func=ACT.Relu)
                nc.sync.dma_start(out=out[P * r : P * (r + 1), 0:N_MAX], in_=o_sb[r][:, 0:N_MAX])
                nc.vector.tensor_scalar(
                    out=o_sb[r][:, N_MAX:F_HID], in0=o_sb[r][:, N_MAX:F_HID], scalar1=0.0, scalar2=None, op0=ALU.max
                )
                nc.sync.dma_start(out=out[P * r : P * (r + 1), N_MAX:F_HID], in_=o_sb[r][:, N_MAX:F_HID])
                return
            nc.scalar.activation(out=o_sb[r][:, 0:n], in_=o_sb[r][:, 0:n], func=ACT.Relu)
            if not TB[r]:
                nc.sync.dma_start(out=out[P * r : P * (r + 1), :], in_=o_sb[r][:])

        def finish_back(r):
            if TB[r]:
                n = direct_end(r)
                copy_back(r, n)

        def copy_back(r, n):
                nc.scalar.copy(
                    out=o_sb[r][:, n:F_HID],
                    in_=back[r][:, PACK - TB[r] : PACK, :].rearrange("p c h -> p (c h)"),
                )
                nc.sync.dma_start(out=out[P * r : P * (r + 1), :], in_=o_sb[r][:])

        xg = {}
        last_r = ROW_TILES - 1

        def ok(r):
            return 0 <= r <= last_r

        def sums(w, ts):
            for t in ts:
                part = None
                if SUMS[w][t] == "P":
                    part = psum_out.tile([P, RS], F32, tag="acc", name="part")
                rowsum(PACK * w + t, part)

        def groups(key):
            for g in range(NODE_PASSES):
                if XG[g] == key:
                    xg[g] = group_x(g)

        def quants(key):
            for g in range(NODE_PASSES):
                if XQ[g] == key:
                    quantise_x(g, xg[g])

        spread_bias()
        groups(0)
        sums(0, (0, 1, 2, 3))
        groups(1)
        quants(0)
        factors(0)
        sums(1, (0, 1))
        groups(2)
        for r in range(4):
            normalise(r, 1)
        if EC:
            factor_cols(4, 6)
        sums(1, (2, 3))
        for r in EC:
            normalise(r, 1)
        quants(1)
        factors(1)
        groups(3)
        sums(2, (0, 1))
        for r in W1A:
            normalise(r, 2)
        quants(2)
        for r in range(4, 6):
            normalise(r, 2)
        quants(3)
        for r in range(6, 8):
            normalise(r, 2)
        sums(2, (2, 3))
        factors(2)
        for r in ET[0]:
            turn_half(r, 0)
            copy_words(r)
        groups(4)
        for r in ET[1]:
            turn_half(r, 0)
            copy_words(r)
        groups(5)
        sums(3, (0, 1, 2))
        for r in W2[0]:
            normalise(r, 3)
        quants(4)
        for r in W2[1]:
            normalise(r, 3)
        quants(5)
        for r in W2[2]:
            normalise(r, 3)
        sums(3, (3,))
        factors(3)
        for r in ET[2]:
            turn_half(r, 0)
            copy_words(r)
        groups(6)
        for r in FILL:
            normalise(r, 3)
        quants(6)
        normalise(0, 4)
        quants(6)
        normalise(1, 4)
        turn(0)
        normalise(2, 4)
        turn(1)
        quants(7)
        for hb in range(HID_BLOCKS):
            turn_w(hb)
        normalise(3, 4)
        quants(7)
        quantise_n(0)

        queue = [(r, g) for r in range(ROW_TILES) for g in range(scaled_to[r], NODE_PASSES)]

        total = len(queue)

        def budget(k):
            want = -(-total * (k + 1) // STEPS)
            return max(0, want - (total - len(queue)))

        def take(n):
            runs = []
            for i in range(n):
                if not queue:
                    break
                r, g = queue.pop(0)
                if runs and runs[-1][0] == r:
                    runs[-1][1] = g + 1
                else:
                    runs.append([r, g + 1])
            return runs

        def step_pieces(k, which):
            if which == 0:
                runs_now.clear()
                runs_now.extend(take(budget(k)))
            for r, hi in runs_now[:1] if which == 0 else runs_now[1:]:
                normalise(r, hi)

        runs_now = []
        ops = {
            "R": relu_turned,
            "A": aggregate,
            "C": copy_agg,
            "Q": quantise_agg,
            "B": lambda r: add_bias(r, 0),
            "b": lambda r: add_bias(r, 1),
            "F": finish,
            "T": turn_mm,
            "W": copy_words,
            "K": turn_back,
            "k": finish_back,
            "H": hidden,
            "N": quantise_n,
        }
        for k in range(FIRST, ROW_TILES + LAST):
            for op, off in ORDER:
                if op == "p" or op == "P":
                    step_pieces(k, 0 if op == "p" else 1)
                elif op == "w":
                    if k == off:
                        quantise_w()
                elif ok(k + off) and (op, k + off) not in HEADDONE:
                    ops[op](k + off)
